import numpy as np
import ml_dtypes


def mxq(x, axis, fmt="e4m3"):
    dtype, down = {"e4m3": (ml_dtypes.float8_e4m3fn, 7), "e5m2": (ml_dtypes.float8_e5m2, 14)}[fmt]
    v = np.moveaxis(np.asarray(x, np.float32).astype(ml_dtypes.bfloat16).astype(np.float64), axis, -1)
    blocks = v.reshape(v.shape[:-1] + (-1, 32))
    amax = np.abs(blocks).max(-1, keepdims=True)
    byte = np.maximum(np.where(amax > 0, np.frexp(amax)[1] - 1 + 127, 0) - down, 1)
    scale = np.exp2(byte - 127.0)
    codes = (blocks / scale).astype(np.float32).astype(dtype).astype(np.float64)
    return np.moveaxis((codes * scale).reshape(v.shape), -1, axis)


WIDE = False


def mx_kscale(k):
    if not WIDE:
        return np.ones(k)
    levels = np.array([10, -10, 5, -5, 0])
    a = np.random.permutation(np.resize(levels, k // 512 * 4)).reshape(k // 512, 4)
    idx = np.arange(k)
    return np.exp2(a[idx // 512, idx % 128 // 32])


BF16 = ml_dtypes.bfloat16


def bf(x):
    return np.asarray(x, np.float32).astype(BF16)


def f64(x):
    return np.asarray(x).astype(np.float64)


B, C, CI, N = 32, 512, 512, 256
A = np.sqrt(0.2 * N / np.sqrt(CI))


def conv1x1(w, b, v):
    return (mxq(w, 1, "e4m3") @ mxq(v, 1, "e4m3")) + b[:, None]


def setup_inputs():
    s, u, t = mx_kscale(C), mx_kscale(C), mx_kscale(CI)
    r = np.random.standard_normal
    return {"x": bf(r((B, C, N)) * s[None, :, None]),
            "x_2": bf(r((B, C, N)) * u[None, :, None]),
            "theta_w": bf(r((CI, C)) * A / np.sqrt(C) * t[:, None] / s[None, :]),
            "theta_b": bf(r(CI) * 0.2 * A * t),
            "phi_w": bf(r((CI, C)) * A / np.sqrt(C) / t[:, None] / u[None, :]),
            "phi_b": bf(r(CI) * 0.2 * A / t)}


def reference(x, x_2, theta_w, theta_b, phi_w, phi_b):
    theta_x = conv1x1(f64(theta_w), f64(theta_b), f64(x)).transpose(0, 2, 1)
    phi_x = conv1x1(f64(phi_w), f64(phi_b), f64(x_2))
    return (mxq(theta_x, 2, "e4m3") @ mxq(phi_x, 1, "e4m3")) / N

@@ -1,0 +1,192 @@
+from contextlib import ExitStack
+
+import concourse.mybir as mybir
+from concourse.masks import make_identity
+
+BF16 = mybir.dt.bfloat16
+F32 = mybir.dt.float32
+U32 = mybir.dt.uint32
+U8 = mybir.dt.uint8
+FP8X4 = mybir.dt.float8_e4m3fn_x4
+IDENTITY = mybir.ActivationFunctionType.Identity
+
+B = 32
+C = 512
+CI = 512
+N = 256
+P = 128
+PACK = 4
+RUN = 4
+ROUND_B = 2
+COLS = ROUND_B * N
+ROUNDS = B // ROUND_B
+POINT_TILES = N // P
+AHEAD = 4
+
+FLOPS = 2 * B * (2 * CI * C * N + N * N * CI)
+
+
+def regroup(nc, grouped, rows):
+    nc.vector.tensor_copy(
+        out=grouped.rearrange("p (c i) t -> p c t i", i=RUN),
+        in_=rows.rearrange("p t (c i) -> p c t i", i=RUN),
+    )
+
+
+def quantise(nc, pool, grouped, cols, name):
+    codes = pool.tile([P, cols], U32, name=name + "_codes", align_bytes=64)
+    scales = pool.tile([P, cols], U8, name=name + "_scales", align_bytes=64)
+    nc.vector.quantize_mx(out=codes[:].bitcast(FP8X4), scales=scales[:], in_=grouped)
+    return codes, scales
+
+
+def tile_sgcam_pa_t_kernel(tc, x, x_2, theta_w, theta_b, phi_w, phi_b, out):
+    nc = tc.nc
+    with ExitStack() as ctx:
+        const = ctx.enter_context(tc.tile_pool(name="const", bufs=1))
+        raw_pool = ctx.enter_context(tc.tile_pool(name="raw", bufs=AHEAD + 1))
+        work = ctx.enter_context(tc.tile_pool(name="work", bufs=2))
+        result_pool = ctx.enter_context(tc.tile_pool(name="result", bufs=3))
+        conv_psum = ctx.enter_context(tc.psum_pool(name="conv_psum", bufs=6))
+        out_psum = ctx.enter_context(tc.psum_pool(name="out_psum", bufs=2))
+
+        def load_points(src, r, name):
+            raw = raw_pool.tile([P, ROUND_B, PACK, N], BF16, name=name + "_raw")
+            nc.sync.dma_start(
+                out=raw[:].rearrange("p b j n -> p b (j n)"),
+                in_=src[r * ROUND_B : (r + 1) * ROUND_B].rearrange(
+                    "b (p j) n -> p b (j n)", j=PACK
+                ),
+            )
+            return raw
+
+        def load_weights(w, name):
+            w_rows = const.tile([P, PACK, C], BF16, name=name + "_rows")
+            nc.sync.dma_start(out=w_rows[:], in_=w.rearrange("(m t) c -> m t c", t=PACK))
+            return w_rows
+
+        def load_bias(b, name):
+            b_bf16 = const.tile([P, PACK], BF16, name=name + "_bf16")
+            nc.scalar.dma_start(out=b_bf16[:], in_=b.rearrange("(m t) -> m t", t=PACK))
+            return b_bf16
+
+        def widen_bias(b_bf16, name):
+            bias = const.tile([P, PACK], F32, name=name + "_f32")
+            nc.vector.tensor_copy(out=bias[:], in_=b_bf16[:])
+            return bias
+
+        def turn_weights(w_rows, name):
+            w_grouped = const.tile([P, PACK * P * PACK], BF16, name=name + "_grouped", align_bytes=64)
+            grouped_words = w_grouped[:].bitcast(F32).rearrange(
+                "q (t m u) -> q t m u", t=PACK, u=2
+            )
+            for half in range(2):
+                turned = conv_psum.tile([P, 2, 2, P], F32, tag="bank")
+                for t2 in range(2):
+                    words = w_rows[:, 2 * half + t2, :].bitcast(F32).rearrange(
+                        "m (q u) -> m u q", u=2
+                    )
+                    for u in range(2):
+                        nc.tensor.transpose(turned[:, t2, u, :], words[:, u, :], ident[:])
+                nc.scalar.copy(
+                    out=grouped_words[:, 2 * half : 2 * half + 2],
+                    in_=turned[:].rearrange("q t u m -> q t m u"),
+                )
+            return w_grouped
+
+        def regroup_points(raw, name):
+            grouped = work.tile([P, ROUND_B, N, PACK], BF16, name=name + "_grouped", align_bytes=64)
+            for b in range(ROUND_B):
+                regroup(nc, grouped[:, b], raw[:, b])
+            return grouped
+
+        def convolve(w_mx, points_mx, bias, name):
+            w_codes, w_scales = w_mx
+            codes, scales = points_mx
+            rows = work.tile([P, PACK, COLS], BF16, name=name + "_rows")
+            for t in range(PACK):
+                bank = conv_psum.tile([P, COLS], F32, tag="bank")
+                nc.tensor.matmul_mx(
+                    out=bank[:],
+                    lhsT=w_codes[:, t * P : (t + 1) * P].bitcast(FP8X4),
+                    lhsT_scale=w_scales[:, t * P : (t + 1) * P],
+                    rhs=codes[:].bitcast(FP8X4),
+                    rhs_scale=scales[:],
+                    start=True,
+                    stop=True,
+                )
+                nc.scalar.activation(
+                    out=rows[:, t, :], in_=bank[:], func=IDENTITY, bias=bias[:, t : t + 1], scale=1.0
+                )
+            return rows
+
+        def quantise_points(x_raw, x2_raw):
+            x_grouped = regroup_points(x_raw, "x")
+            x2_grouped = regroup_points(x2_raw, "x2")
+            x_mx = quantise(nc, work, x_grouped[:].rearrange("p b n t -> p (b n t)"), COLS, "x")
+            x2_mx = quantise(nc, work, x2_grouped[:].rearrange("p b n t -> p (b n t)"), COLS, "x2")
+            return x_mx, x2_mx
+
+        def affinity(r, theta_rows, phi_rows):
+            theta_grouped = work.tile([P, COLS, PACK], BF16, name="theta_grouped", align_bytes=64)
+            phi_grouped = work.tile([P, COLS, PACK], BF16, name="phi_grouped", align_bytes=64)
+            regroup(nc, theta_grouped[:], theta_rows[:])
+            regroup(nc, phi_grouped[:], phi_rows[:])
+            theta_codes, theta_scales = quantise(
+                nc, work, theta_grouped[:].rearrange("p c t -> p (c t)"), COLS, "theta"
+            )
+            phi_codes, phi_scales = quantise(
+                nc, work, phi_grouped[:].rearrange("p c t -> p (c t)"), COLS, "phi"
+            )
+            result = result_pool.tile([P, ROUND_B, POINT_TILES, N], F32, name="result")
+            for b in range(ROUND_B):
+                product = out_psum.tile([P, POINT_TILES, N], F32, name="product")
+                for i in range(POINT_TILES):
+                    first = b * N + i * P
+                    nc.tensor.matmul_mx(
+                        out=product[:, i, :],
+                        lhsT=theta_codes[:, first : first + P].bitcast(FP8X4),
+                        lhsT_scale=theta_scales[:, first : first + P],
+                        rhs=phi_codes[:, b * N : (b + 1) * N].bitcast(FP8X4),
+                        rhs_scale=phi_scales[:, b * N : (b + 1) * N],
+                        start=True,
+                        stop=True,
+                    )
+                nc.scalar.mul(out=result[:, b], in_=product[:], mul=1.0 / N)
+            nc.sync.dma_start(
+                out=out[r * ROUND_B : (r + 1) * ROUND_B].rearrange("b (i p) m -> p (b i) m", p=P),
+                in_=result[:].rearrange("p b i m -> p (b i) m"),
+            )
+
+        x_raws = [load_points(x, 0, "x")]
+        x2_raws = [load_points(x_2, 0, "x2")]
+        theta_w_rows = load_weights(theta_w, "theta_w")
+        phi_w_rows = load_weights(phi_w, "phi_w")
+        theta_b_bf16 = load_bias(theta_b, "theta_b")
+        phi_b_bf16 = load_bias(phi_b, "phi_b")
+        for r in range(1, AHEAD):
+            x_raws.append(load_points(x, r, "x"))
+            x2_raws.append(load_points(x_2, r, "x2"))
+
+        ident = const.tile([P, P], F32, name="ident")
+        make_identity(nc, ident[:])
+        theta_w_grouped = turn_weights(theta_w_rows, "theta_w")
+        phi_w_grouped = turn_weights(phi_w_rows, "phi_w")
+
+        waiting = None
+        for r in range(ROUNDS):
+            if r + AHEAD < ROUNDS:
+                x_raws.append(load_points(x, r + AHEAD, "x"))
+                x2_raws.append(load_points(x_2, r + AHEAD, "x2"))
+            x_mx, x2_mx = quantise_points(x_raws[r], x2_raws[r])
+            if r == 0:
+                theta_bias = widen_bias(theta_b_bf16, "theta_b")
+                phi_bias = widen_bias(phi_b_bf16, "phi_b")
+                theta_w_mx = quantise(nc, const, theta_w_grouped[:], PACK * P, "theta_w")
+                phi_w_mx = quantise(nc, const, phi_w_grouped[:], PACK * P, "phi_w")
+            theta_rows = convolve(theta_w_mx, x_mx, theta_bias, "theta")
+            phi_rows = convolve(phi_w_mx, x2_mx, phi_bias, "phi")
+            if waiting is not None:
+                affinity(r - 1, waiting[0], waiting[1])
+            waiting = (theta_rows, phi_rows)
+        affinity(ROUNDS - 1, waiting[0], waiting[1])

@@ -22,12 +22,14 @@ COLS = ROUND_B * N
 ROUNDS = B // ROUND_B
 POINT_TILES = N // P
 AHEAD = 4
+SCALAR_COLS = 160
+VECTOR_COLS = COLS - SCALAR_COLS
 
 FLOPS = 2 * B * (2 * CI * C * N + N * N * CI)
 
 
-def regroup(nc, grouped, rows):
-    nc.vector.tensor_copy(
+def regroup(copy, grouped, rows):
+    copy(
         out=grouped.rearrange("p (c i) t -> p c t i", i=RUN),
         in_=rows.rearrange("p t (c i) -> p c t i", i=RUN),
     )
@@ -97,7 +99,7 @@ def tile_sgcam_pa_t_kernel(tc, x, x_2, theta_w, theta_b, phi_w, phi_b, out):
         def regroup_points(raw, name):
             grouped = work.tile([P, ROUND_B, N, PACK], BF16, name=name + "_grouped", align_bytes=64)
             for b in range(ROUND_B):
-                regroup(nc, grouped[:, b], raw[:, b])
+                regroup(nc.vector.tensor_copy, grouped[:, b], raw[:, b])
             return grouped
 
         def convolve(w_mx, points_mx, bias, name):
@@ -127,11 +129,17 @@ def tile_sgcam_pa_t_kernel(tc, x, x_2, theta_w, theta_b, phi_w, phi_b, out):
             x2_mx = quantise(nc, work, x2_grouped[:].rearrange("p b n t -> p (b n t)"), COLS, "x2")
             return x_mx, x2_mx
 
-        def affinity(r, theta_rows, phi_rows):
-            theta_grouped = work.tile([P, COLS, PACK], BF16, name="theta_grouped", align_bytes=64)
+        def start_phi_grouped(phi_rows):
             phi_grouped = work.tile([P, COLS, PACK], BF16, name="phi_grouped", align_bytes=64)
-            regroup(nc, theta_grouped[:], theta_rows[:])
-            regroup(nc, phi_grouped[:], phi_rows[:])
+            regroup(nc.scalar.copy, phi_grouped[:, VECTOR_COLS:, :], phi_rows[:, :, VECTOR_COLS:])
+            return phi_grouped
+
+        def affinity(r, theta_rows, phi_rows, phi_grouped):
+            theta_grouped = work.tile([P, COLS, PACK], BF16, name="theta_grouped", align_bytes=64)
+            regroup(nc.vector.tensor_copy, theta_grouped[:], theta_rows[:])
+            regroup(
+                nc.vector.tensor_copy, phi_grouped[:, :VECTOR_COLS, :], phi_rows[:, :, :VECTOR_COLS]
+            )
             theta_codes, theta_scales = quantise(
                 nc, work, theta_grouped[:].rearrange("p c t -> p (c t)"), COLS, "theta"
             )
@@ -186,7 +194,8 @@ def tile_sgcam_pa_t_kernel(tc, x, x_2, theta_w, theta_b, phi_w, phi_b, out):
                 phi_w_mx = quantise(nc, const, phi_w_grouped[:], PACK * P, "phi_w")
             theta_rows = convolve(theta_w_mx, x_mx, theta_bias, "theta")
             phi_rows = convolve(phi_w_mx, x2_mx, phi_bias, "phi")
+            phi_grouped = start_phi_grouped(phi_rows)
             if waiting is not None:
-                affinity(r - 1, waiting[0], waiting[1])
-            waiting = (theta_rows, phi_rows)
-        affinity(ROUNDS - 1, waiting[0], waiting[1])
+                affinity(r - 1, waiting[0], waiting[1], waiting[2])
+            waiting = (theta_rows, phi_rows, phi_grouped)
+        affinity(ROUNDS - 1, waiting[0], waiting[1], waiting[2])

@@ -9,6 +9,8 @@ U32 = mybir.dt.uint32
 U8 = mybir.dt.uint8
 FP8X4 = mybir.dt.float8_e4m3fn_x4
 IDENTITY = mybir.ActivationFunctionType.Identity
+ADD = mybir.AluOpType.add
+MULT = mybir.AluOpType.mult
 
 B = 32
 C = 512
@@ -20,19 +22,14 @@ RUN = 4
 ROUND_B = 2
 COLS = ROUND_B * N
 ROUNDS = B // ROUND_B
-POINT_TILES = N // P
-AHEAD = 4
-SCALAR_COLS = 160
-VECTOR_COLS = COLS - SCALAR_COLS
+TILES = COLS // P
+BATCH_TILES = N // P
+SCALAR_TILES = 2
+VECTOR_TILES = TILES - SCALAR_TILES
+REGROUP_AHEAD = 2
+LOAD_AHEAD = 5
 
 FLOPS = 2 * B * (2 * CI * C * N + N * N * CI)
-
-
-def regroup(copy, grouped, rows):
-    copy(
-        out=grouped.rearrange("p (c i) t -> p c t i", i=RUN),
-        in_=rows.rearrange("p t (c i) -> p c t i", i=RUN),
-    )
 
 
 def quantise(nc, pool, grouped, cols, name):
@@ -46,7 +43,8 @@ def tile_sgcam_pa_t_kernel(tc, x, x_2, theta_w, theta_b, phi_w, phi_b, out):
     nc = tc.nc
     with ExitStack() as ctx:
         const = ctx.enter_context(tc.tile_pool(name="const", bufs=1))
-        raw_pool = ctx.enter_context(tc.tile_pool(name="raw", bufs=AHEAD + 1))
+        raw_pool = ctx.enter_context(tc.tile_pool(name="raw", bufs=LOAD_AHEAD))
+        front = ctx.enter_context(tc.tile_pool(name="front", bufs=REGROUP_AHEAD + 1))
         work = ctx.enter_context(tc.tile_pool(name="work", bufs=2))
         result_pool = ctx.enter_context(tc.tile_pool(name="result", bufs=3))
         conv_psum = ctx.enter_context(tc.psum_pool(name="conv_psum", bufs=6))
@@ -77,7 +75,7 @@ def tile_sgcam_pa_t_kernel(tc, x, x_2, theta_w, theta_b, phi_w, phi_b, out):
             nc.vector.tensor_copy(out=bias[:], in_=b_bf16[:])
             return bias
 
-        def turn_weights(w_rows, name):
+        def quantise_weights(w_rows, name):
             w_grouped = const.tile([P, PACK * P * PACK], BF16, name=name + "_grouped", align_bytes=64)
             grouped_words = w_grouped[:].bitcast(F32).rearrange(
                 "q (t m u) -> q t m u", t=PACK, u=2
@@ -90,66 +88,71 @@ def tile_sgcam_pa_t_kernel(tc, x, x_2, theta_w, theta_b, phi_w, phi_b, out):
                     )
                     for u in range(2):
                         nc.tensor.transpose(turned[:, t2, u, :], words[:, u, :], ident[:])
-                nc.scalar.copy(
+                nc.vector.tensor_copy(
                     out=grouped_words[:, 2 * half : 2 * half + 2],
                     in_=turned[:].rearrange("q t u m -> q t m u"),
                 )
-            return w_grouped
+            return quantise(nc, const, w_grouped[:], PACK * P, name)
 
-        def regroup_points(raw, name):
-            grouped = work.tile([P, ROUND_B, N, PACK], BF16, name=name + "_grouped", align_bytes=64)
+        def regroup_points(x_raw, x2_raw):
+            x_grouped = front.tile([P, ROUND_B, N, PACK], BF16, name="x_grouped", align_bytes=64)
+            x2_grouped = front.tile([P, ROUND_B, N, PACK], BF16, name="x2_grouped", align_bytes=64)
             for b in range(ROUND_B):
-                regroup(nc.vector.tensor_copy, grouped[:, b], raw[:, b])
-            return grouped
+                nc.scalar.copy(
+                    out=x_grouped[:, b].rearrange("p (c i) j -> p c j i", i=RUN),
+                    in_=x_raw[:, b].rearrange("p j (c i) -> p c j i", i=RUN),
+                )
+                nc.gpsimd.tensor_scalar(
+                    out=x2_grouped[:, b],
+                    in0=x2_raw[:, b].rearrange("p j n -> p n j"),
+                    scalar1=1.0,
+                    scalar2=0.0,
+                    op0=MULT,
+                    op1=ADD,
+                )
+            return x_grouped, x2_grouped
 
-        def convolve(w_mx, points_mx, bias, name):
+        def project_tile(w_mx, points_mx, i):
             w_codes, w_scales = w_mx
             codes, scales = points_mx
-            rows = work.tile([P, PACK, COLS], BF16, name=name + "_rows")
+            bank = conv_psum.tile([P, PACK, P], F32, tag="bank")
             for t in range(PACK):
-                bank = conv_psum.tile([P, COLS], F32, tag="bank")
                 nc.tensor.matmul_mx(
-                    out=bank[:],
+                    out=bank[:, t, :],
                     lhsT=w_codes[:, t * P : (t + 1) * P].bitcast(FP8X4),
                     lhsT_scale=w_scales[:, t * P : (t + 1) * P],
-                    rhs=codes[:].bitcast(FP8X4),
-                    rhs_scale=scales[:],
+                    rhs=codes[:, i * P : (i + 1) * P].bitcast(FP8X4),
+                    rhs_scale=scales[:, i * P : (i + 1) * P],
                     start=True,
                     stop=True,
                 )
+            return bank
+
+        def vector_empties(bank, bias, grouped, i):
+            nc.vector.tensor_tensor(
+                out=grouped[:, i * P : (i + 1) * P, :],
+                in0=bank[:].rearrange("m t n -> m n t"),
+                in1=bias[:].unsqueeze(1).to_broadcast([P, P, PACK]),
+                op=ADD,
+            )
+
+        def scalar_empties(bank, bias, rows, i):
+            for t in range(PACK):
                 nc.scalar.activation(
-                    out=rows[:, t, :], in_=bank[:], func=IDENTITY, bias=bias[:, t : t + 1], scale=1.0
+                    out=rows[:, t, i * P : (i + 1) * P],
+                    in_=bank[:, t, :],
+                    func=IDENTITY,
+                    bias=bias[:, t : t + 1],
+                    scale=1.0,
                 )
-            return rows
 
-        def quantise_points(x_raw, x2_raw):
-            x_grouped = regroup_points(x_raw, "x")
-            x2_grouped = regroup_points(x2_raw, "x2")
-            x_mx = quantise(nc, work, x_grouped[:].rearrange("p b n t -> p (b n t)"), COLS, "x")
-            x2_mx = quantise(nc, work, x2_grouped[:].rearrange("p b n t -> p (b n t)"), COLS, "x2")
-            return x_mx, x2_mx
-
-        def start_phi_grouped(phi_rows):
-            phi_grouped = work.tile([P, COLS, PACK], BF16, name="phi_grouped", align_bytes=64)
-            regroup(nc.scalar.copy, phi_grouped[:, VECTOR_COLS:, :], phi_rows[:, :, VECTOR_COLS:])
-            return phi_grouped
-
-        def affinity(r, theta_rows, phi_rows, phi_grouped):
-            theta_grouped = work.tile([P, COLS, PACK], BF16, name="theta_grouped", align_bytes=64)
-            regroup(nc.vector.tensor_copy, theta_grouped[:], theta_rows[:])
-            regroup(
-                nc.vector.tensor_copy, phi_grouped[:, :VECTOR_COLS, :], phi_rows[:, :, :VECTOR_COLS]
-            )
-            theta_codes, theta_scales = quantise(
-                nc, work, theta_grouped[:].rearrange("p c t -> p (c t)"), COLS, "theta"
-            )
-            phi_codes, phi_scales = quantise(
-                nc, work, phi_grouped[:].rearrange("p c t -> p (c t)"), COLS, "phi"
-            )
-            result = result_pool.tile([P, ROUND_B, POINT_TILES, N], F32, name="result")
+        def affinity(r, theta_mx, phi_mx):
+            theta_codes, theta_scales = theta_mx
+            phi_codes, phi_scales = phi_mx
+            result = result_pool.tile([P, ROUND_B, BATCH_TILES, N], F32, name="result")
             for b in range(ROUND_B):
-                product = out_psum.tile([P, POINT_TILES, N], F32, name="product")
-                for i in range(POINT_TILES):
+                product = out_psum.tile([P, BATCH_TILES, N], F32, name="product")
+                for i in range(BATCH_TILES):
                     first = b * N + i * P
                     nc.tensor.matmul_mx(
                         out=product[:, i, :],
@@ -166,36 +169,54 @@ def tile_sgcam_pa_t_kernel(tc, x, x_2, theta_w, theta_b, phi_w, phi_b, out):
                 in_=result[:].rearrange("p b i m -> p (b i) m"),
             )
 
-        x_raws = [load_points(x, 0, "x")]
         x2_raws = [load_points(x_2, 0, "x2")]
-        theta_w_rows = load_weights(theta_w, "theta_w")
+        x_raws = [load_points(x, 0, "x")]
         phi_w_rows = load_weights(phi_w, "phi_w")
-        theta_b_bf16 = load_bias(theta_b, "theta_b")
+        theta_w_rows = load_weights(theta_w, "theta_w")
         phi_b_bf16 = load_bias(phi_b, "phi_b")
-        for r in range(1, AHEAD):
-            x_raws.append(load_points(x, r, "x"))
+        theta_b_bf16 = load_bias(theta_b, "theta_b")
+        for r in range(1, LOAD_AHEAD):
             x2_raws.append(load_points(x_2, r, "x2"))
+            x_raws.append(load_points(x, r, "x"))
 
         ident = const.tile([P, P], F32, name="ident")
         make_identity(nc, ident[:])
-        theta_w_grouped = turn_weights(theta_w_rows, "theta_w")
-        phi_w_grouped = turn_weights(phi_w_rows, "phi_w")
+        grouped_points = [regroup_points(x_raws[r], x2_raws[r]) for r in range(REGROUP_AHEAD)]
+        phi_w_mx = quantise_weights(phi_w_rows, "phi_w")
+        theta_w_mx = quantise_weights(theta_w_rows, "theta_w")
+        phi_bias = widen_bias(phi_b_bf16, "phi_b")
+        theta_bias = widen_bias(theta_b_bf16, "theta_b")
 
-        waiting = None
         for r in range(ROUNDS):
-            if r + AHEAD < ROUNDS:
-                x_raws.append(load_points(x, r + AHEAD, "x"))
-                x2_raws.append(load_points(x_2, r + AHEAD, "x2"))
-            x_mx, x2_mx = quantise_points(x_raws[r], x2_raws[r])
-            if r == 0:
-                theta_bias = widen_bias(theta_b_bf16, "theta_b")
-                phi_bias = widen_bias(phi_b_bf16, "phi_b")
-                theta_w_mx = quantise(nc, const, theta_w_grouped[:], PACK * P, "theta_w")
-                phi_w_mx = quantise(nc, const, phi_w_grouped[:], PACK * P, "phi_w")
-            theta_rows = convolve(theta_w_mx, x_mx, theta_bias, "theta")
-            phi_rows = convolve(phi_w_mx, x2_mx, phi_bias, "phi")
-            phi_grouped = start_phi_grouped(phi_rows)
-            if waiting is not None:
-                affinity(r - 1, waiting[0], waiting[1], waiting[2])
-            waiting = (theta_rows, phi_rows, phi_grouped)
-        affinity(ROUNDS - 1, waiting[0], waiting[1], waiting[2])
+            if r + LOAD_AHEAD < ROUNDS:
+                x2_raws.append(load_points(x_2, r + LOAD_AHEAD, "x2"))
+                x_raws.append(load_points(x, r + LOAD_AHEAD, "x"))
+            x_grouped, x2_grouped = grouped_points[r]
+            x2_mx = quantise(nc, work, x2_grouped[:].rearrange("p b n j -> p (b n j)"), COLS, "x2")
+            x_mx = quantise(nc, work, x_grouped[:].rearrange("p b n j -> p (b n j)"), COLS, "x")
+
+            theta_grouped = work.tile([P, COLS, PACK], BF16, name="theta_grouped", align_bytes=64)
+            phi_grouped = work.tile([P, COLS, PACK], BF16, name="phi_grouped", align_bytes=64)
+            phi_rows = work.tile([P, PACK, SCALAR_TILES * P], BF16, name="phi_rows")
+            for i in range(SCALAR_TILES):
+                bank = project_tile(phi_w_mx, x2_mx, VECTOR_TILES + i)
+                scalar_empties(bank, phi_bias, phi_rows, i)
+            nc.scalar.copy(
+                out=phi_grouped[:, VECTOR_TILES * P :, :].rearrange("m (c i) t -> m c t i", i=RUN),
+                in_=phi_rows[:].rearrange("m t (c i) -> m c t i", i=RUN),
+            )
+            for i in range(VECTOR_TILES):
+                bank = project_tile(phi_w_mx, x2_mx, i)
+                vector_empties(bank, phi_bias, phi_grouped, i)
+            for i in range(TILES):
+                bank = project_tile(theta_w_mx, x_mx, i)
+                vector_empties(bank, theta_bias, theta_grouped, i)
+
+            if r + REGROUP_AHEAD < ROUNDS:
+                grouped_points.append(
+                    regroup_points(x_raws[r + REGROUP_AHEAD], x2_raws[r + REGROUP_AHEAD])
+                )
+
+            phi_mx = quantise(nc, work, phi_grouped[:].rearrange("m c t -> m (c t)"), COLS, "phi")
+            theta_mx = quantise(nc, work, theta_grouped[:].rearrange("m c t -> m (c t)"), COLS, "theta")
+            affinity(r, theta_mx, phi_mx)

@@ -187,13 +187,17 @@ def tile_sgcam_pa_t_kernel(tc, x, x_2, theta_w, theta_b, phi_w, phi_b, out):
         phi_bias = widen_bias(phi_b_bf16, "phi_b")
         theta_bias = widen_bias(theta_b_bf16, "theta_b")
 
+        def quantise_points(r):
+            x_grouped, x2_grouped = grouped_points[r]
+            x2_mx = quantise(nc, work, x2_grouped[:].rearrange("p b n j -> p (b n j)"), COLS, "x2")
+            x_mx = quantise(nc, work, x_grouped[:].rearrange("p b n j -> p (b n j)"), COLS, "x")
+            return x_mx, x2_mx
+
+        x_mx, x2_mx = quantise_points(0)
         for r in range(ROUNDS):
             if r + LOAD_AHEAD < ROUNDS:
                 x2_raws.append(load_points(x_2, r + LOAD_AHEAD, "x2"))
                 x_raws.append(load_points(x, r + LOAD_AHEAD, "x"))
-            x_grouped, x2_grouped = grouped_points[r]
-            x2_mx = quantise(nc, work, x2_grouped[:].rearrange("p b n j -> p (b n j)"), COLS, "x2")
-            x_mx = quantise(nc, work, x_grouped[:].rearrange("p b n j -> p (b n j)"), COLS, "x")
 
             theta_grouped = work.tile([P, COLS, PACK], BF16, name="theta_grouped", align_bytes=64)
             phi_grouped = work.tile([P, COLS, PACK], BF16, name="phi_grouped", align_bytes=64)
@@ -217,6 +221,8 @@ def tile_sgcam_pa_t_kernel(tc, x, x_2, theta_w, theta_b, phi_w, phi_b, out):
                     regroup_points(x_raws[r + REGROUP_AHEAD], x2_raws[r + REGROUP_AHEAD])
                 )
 
+            if r + 1 < ROUNDS:
+                x_mx, x2_mx = quantise_points(r + 1)
             phi_mx = quantise(nc, work, phi_grouped[:].rearrange("m c t -> m (c t)"), COLS, "phi")
             theta_mx = quantise(nc, work, theta_grouped[:].rearrange("m c t -> m (c t)"), COLS, "theta")
             affinity(r, theta_mx, phi_mx)

@@ -26,8 +26,9 @@ TILES = COLS // P
 BATCH_TILES = N // P
 SCALAR_TILES = 2
 VECTOR_TILES = TILES - SCALAR_TILES
-REGROUP_AHEAD = 2
-LOAD_AHEAD = 5
+REGROUP_AHEAD = 3
+QUANTISE_AHEAD = 2
+LOAD_AHEAD = 6
 
 FLOPS = 2 * B * (2 * CI * C * N + N * N * CI)
 
@@ -45,6 +46,8 @@ def tile_sgcam_pa_t_kernel(tc, x, x_2, theta_w, theta_b, phi_w, phi_b, out):
         const = ctx.enter_context(tc.tile_pool(name="const", bufs=1))
         raw_pool = ctx.enter_context(tc.tile_pool(name="raw", bufs=LOAD_AHEAD))
         front = ctx.enter_context(tc.tile_pool(name="front", bufs=REGROUP_AHEAD + 1))
+        x2_front = ctx.enter_context(tc.tile_pool(name="x2_front", bufs=2))
+        points_mx_pool = ctx.enter_context(tc.tile_pool(name="points_mx", bufs=QUANTISE_AHEAD + 1))
         work = ctx.enter_context(tc.tile_pool(name="work", bufs=2))
         result_pool = ctx.enter_context(tc.tile_pool(name="result", bufs=3))
         conv_psum = ctx.enter_context(tc.psum_pool(name="conv_psum", bufs=6))
@@ -96,7 +99,7 @@ def tile_sgcam_pa_t_kernel(tc, x, x_2, theta_w, theta_b, phi_w, phi_b, out):
 
         def regroup_points(x_raw, x2_raw):
             x_grouped = front.tile([P, ROUND_B, N, PACK], BF16, name="x_grouped", align_bytes=64)
-            x2_grouped = front.tile([P, ROUND_B, N, PACK], BF16, name="x2_grouped", align_bytes=64)
+            x2_grouped = x2_front.tile([P, ROUND_B, N, PACK], BF16, name="x2_grouped", align_bytes=64)
             for b in range(ROUND_B):
                 nc.scalar.copy(
                     out=x_grouped[:, b].rearrange("p (c i) j -> p c j i", i=RUN),
@@ -187,13 +190,17 @@ def tile_sgcam_pa_t_kernel(tc, x, x_2, theta_w, theta_b, phi_w, phi_b, out):
         phi_bias = widen_bias(phi_b_bf16, "phi_b")
         theta_bias = widen_bias(theta_b_bf16, "theta_b")
 
-        def quantise_points(r):
-            x_grouped, x2_grouped = grouped_points[r]
-            x2_mx = quantise(nc, work, x2_grouped[:].rearrange("p b n j -> p (b n j)"), COLS, "x2")
-            x_mx = quantise(nc, work, x_grouped[:].rearrange("p b n j -> p (b n j)"), COLS, "x")
-            return x_mx, x2_mx
+        def quantise_x(r):
+            grouped = grouped_points[r][0][:].rearrange("p b n j -> p (b n j)")
+            return quantise(nc, points_mx_pool, grouped, COLS, "x")
 
-        x_mx, x2_mx = quantise_points(0)
+        def quantise_x2(r):
+            grouped = grouped_points[r][1][:].rearrange("p b n j -> p (b n j)")
+            return quantise(nc, points_mx_pool, grouped, COLS, "x2")
+
+        ctx.enter_context(tc.manual_schedule(engines={mybir.EngineType.DVE}))
+        x_mx = {0: quantise_x(0)}
+        x2_mx = {0: quantise_x2(0)}
         for r in range(ROUNDS):
             if r + LOAD_AHEAD < ROUNDS:
                 x2_raws.append(load_points(x_2, r + LOAD_AHEAD, "x2"))
@@ -203,17 +210,17 @@ def tile_sgcam_pa_t_kernel(tc, x, x_2, theta_w, theta_b, phi_w, phi_b, out):
             phi_grouped = work.tile([P, COLS, PACK], BF16, name="phi_grouped", align_bytes=64)
             phi_rows = work.tile([P, PACK, SCALAR_TILES * P], BF16, name="phi_rows")
             for i in range(SCALAR_TILES):
-                bank = project_tile(phi_w_mx, x2_mx, VECTOR_TILES + i)
+                bank = project_tile(phi_w_mx, x2_mx[r], VECTOR_TILES + i)
                 scalar_empties(bank, phi_bias, phi_rows, i)
             nc.scalar.copy(
                 out=phi_grouped[:, VECTOR_TILES * P :, :].rearrange("m (c i) t -> m c t i", i=RUN),
                 in_=phi_rows[:].rearrange("m t (c i) -> m c t i", i=RUN),
             )
             for i in range(VECTOR_TILES):
-                bank = project_tile(phi_w_mx, x2_mx, i)
+                bank = project_tile(phi_w_mx, x2_mx[r], i)
                 vector_empties(bank, phi_bias, phi_grouped, i)
             for i in range(TILES):
-                bank = project_tile(theta_w_mx, x_mx, i)
+                bank = project_tile(theta_w_mx, x_mx[r], i)
                 vector_empties(bank, theta_bias, theta_grouped, i)
 
             if r + REGROUP_AHEAD < ROUNDS:
@@ -221,8 +228,14 @@ def tile_sgcam_pa_t_kernel(tc, x, x_2, theta_w, theta_b, phi_w, phi_b, out):
                     regroup_points(x_raws[r + REGROUP_AHEAD], x2_raws[r + REGROUP_AHEAD])
                 )
 
-            if r + 1 < ROUNDS:
-                x_mx, x2_mx = quantise_points(r + 1)
+            if r == 0:
+                x_mx[1] = quantise_x(1)
+                x2_mx[1] = quantise_x2(1)
+            ahead = r + QUANTISE_AHEAD
             phi_mx = quantise(nc, work, phi_grouped[:].rearrange("m c t -> m (c t)"), COLS, "phi")
+            if ahead < ROUNDS:
+                x_mx[ahead] = quantise_x(ahead)
             theta_mx = quantise(nc, work, theta_grouped[:].rearrange("m c t -> m (c t)"), COLS, "theta")
+            if ahead < ROUNDS:
+                x2_mx[ahead] = quantise_x2(ahead)
             affinity(r, theta_mx, phi_mx)

@@ -55,12 +55,14 @@ def tile_sgcam_pa_t_kernel(tc, x, x_2, theta_w, theta_b, phi_w, phi_b, out):
 
         def load_points(src, r, name):
             raw = raw_pool.tile([P, ROUND_B, PACK, N], BF16, name=name + "_raw")
-            nc.sync.dma_start(
-                out=raw[:].rearrange("p b j n -> p b (j n)"),
-                in_=src[r * ROUND_B : (r + 1) * ROUND_B].rearrange(
-                    "b (p j) n -> p b (j n)", j=PACK
-                ),
-            )
+            step = 1 if r == 0 else ROUND_B
+            for b in range(0, ROUND_B, step):
+                nc.sync.dma_start(
+                    out=raw[:, b : b + step].rearrange("p b j n -> p b (j n)"),
+                    in_=src[r * ROUND_B + b : r * ROUND_B + b + step].rearrange(
+                        "b (p j) n -> p b (j n)", j=PACK
+                    ),
+                )
             return raw
 
         def load_weights(w, name):
@@ -78,7 +80,7 @@ def tile_sgcam_pa_t_kernel(tc, x, x_2, theta_w, theta_b, phi_w, phi_b, out):
             nc.vector.tensor_copy(out=bias[:], in_=b_bf16[:])
             return bias
 
-        def quantise_weights(w_rows, name):
+        def turn_weights(w_rows, copies, name):
             w_grouped = const.tile([P, PACK * P * PACK], BF16, name=name + "_grouped", align_bytes=64)
             grouped_words = w_grouped[:].bitcast(F32).rearrange(
                 "q (t m u) -> q t m u", t=PACK, u=2
@@ -91,29 +93,40 @@ def tile_sgcam_pa_t_kernel(tc, x, x_2, theta_w, theta_b, phi_w, phi_b, out):
                     )
                     for u in range(2):
                         nc.tensor.transpose(turned[:, t2, u, :], words[:, u, :], ident[:])
-                nc.vector.tensor_copy(
+                copies[half](
                     out=grouped_words[:, 2 * half : 2 * half + 2],
                     in_=turned[:].rearrange("q t u m -> q t m u"),
                 )
-            return quantise(nc, const, w_grouped[:], PACK * P, name)
+            return w_grouped
 
-        def regroup_points(x_raw, x2_raw):
-            x_grouped = front.tile([P, ROUND_B, N, PACK], BF16, name="x_grouped", align_bytes=64)
-            x2_grouped = x2_front.tile([P, ROUND_B, N, PACK], BF16, name="x2_grouped", align_bytes=64)
+        def regroup_x_batch(r, b):
+            if b == 0:
+                x_grouped.append(
+                    front.tile([P, ROUND_B, N, PACK], BF16, name="x_grouped", align_bytes=64)
+                )
+            nc.scalar.copy(
+                out=x_grouped[r][:, b].rearrange("p (c i) j -> p c j i", i=RUN),
+                in_=x_raws[r][:, b].rearrange("p j (c i) -> p c j i", i=RUN),
+            )
+
+        def regroup_x2(r):
+            grouped = x2_front.tile([P, ROUND_B, N, PACK], BF16, name="x2_grouped", align_bytes=64)
             for b in range(ROUND_B):
-                nc.scalar.copy(
-                    out=x_grouped[:, b].rearrange("p (c i) j -> p c j i", i=RUN),
-                    in_=x_raw[:, b].rearrange("p j (c i) -> p c j i", i=RUN),
-                )
-                nc.gpsimd.tensor_scalar(
-                    out=x2_grouped[:, b],
-                    in0=x2_raw[:, b].rearrange("p j n -> p n j"),
-                    scalar1=1.0,
-                    scalar2=0.0,
-                    op0=MULT,
-                    op1=ADD,
-                )
-            return x_grouped, x2_grouped
+                if r == 0 and b == 0:
+                    nc.vector.tensor_copy(
+                        out=grouped[:, b].rearrange("p (c i) j -> p c j i", i=RUN),
+                        in_=x2_raws[r][:, b].rearrange("p j (c i) -> p c j i", i=RUN),
+                    )
+                else:
+                    nc.gpsimd.tensor_scalar(
+                        out=grouped[:, b],
+                        in0=x2_raws[r][:, b].rearrange("p j n -> p n j"),
+                        scalar1=1.0,
+                        scalar2=0.0,
+                        op0=MULT,
+                        op1=ADD,
+                    )
+            x2_grouped.append(grouped)
 
         def project_tile(w_mx, points_mx, i):
             w_codes, w_scales = w_mx
@@ -149,10 +162,10 @@ def tile_sgcam_pa_t_kernel(tc, x, x_2, theta_w, theta_b, phi_w, phi_b, out):
                     scale=1.0,
                 )
 
-        def affinity(r, theta_mx, phi_mx):
+        def affinity(theta_mx, phi_mx):
             theta_codes, theta_scales = theta_mx
             phi_codes, phi_scales = phi_mx
-            result = result_pool.tile([P, ROUND_B, BATCH_TILES, N], F32, name="result")
+            products = []
             for b in range(ROUND_B):
                 product = out_psum.tile([P, BATCH_TILES, N], F32, name="product")
                 for i in range(BATCH_TILES):
@@ -166,41 +179,65 @@ def tile_sgcam_pa_t_kernel(tc, x, x_2, theta_w, theta_b, phi_w, phi_b, out):
                         start=True,
                         stop=True,
                     )
-                nc.scalar.mul(out=result[:, b], in_=product[:], mul=1.0 / N)
+                products.append(product)
+            return products
+
+        def store(r, result):
             nc.sync.dma_start(
                 out=out[r * ROUND_B : (r + 1) * ROUND_B].rearrange("b (i p) m -> p (b i) m", p=P),
                 in_=result[:].rearrange("p b i m -> p (b i) m"),
             )
 
-        x2_raws = [load_points(x_2, 0, "x2")]
-        x_raws = [load_points(x, 0, "x")]
-        phi_w_rows = load_weights(phi_w, "phi_w")
-        theta_w_rows = load_weights(theta_w, "theta_w")
+        def finish(r, theta_mx, phi_mx, x_round):
+            products = affinity(theta_mx, phi_mx)
+            result = result_pool.tile([P, ROUND_B, BATCH_TILES, N], F32, name="result")
+            for b in range(ROUND_B):
+                if x_round < ROUNDS:
+                    regroup_x_batch(x_round, b)
+                nc.scalar.mul(out=result[:, b], in_=products[b][:], mul=1.0 / N)
+            store(r, result)
+
+
+        ctx.enter_context(
+            tc.manual_schedule(
+                engines={mybir.EngineType.DVE, mybir.EngineType.Activation, mybir.EngineType.PE}
+            )
+        )
         phi_b_bf16 = load_bias(phi_b, "phi_b")
         theta_b_bf16 = load_bias(theta_b, "theta_b")
+        phi_w_rows = load_weights(phi_w, "phi_w")
+        x2_raws = [load_points(x_2, 0, "x2")]
+        theta_w_rows = load_weights(theta_w, "theta_w")
+        x_raws = [load_points(x, 0, "x")]
         for r in range(1, LOAD_AHEAD):
             x2_raws.append(load_points(x_2, r, "x2"))
             x_raws.append(load_points(x, r, "x"))
 
         ident = const.tile([P, P], F32, name="ident")
         make_identity(nc, ident[:])
-        grouped_points = [regroup_points(x_raws[r], x2_raws[r]) for r in range(REGROUP_AHEAD)]
-        phi_w_mx = quantise_weights(phi_w_rows, "phi_w")
-        theta_w_mx = quantise_weights(theta_w_rows, "theta_w")
-        phi_bias = widen_bias(phi_b_bf16, "phi_b")
-        theta_bias = widen_bias(theta_b_bf16, "theta_b")
+        x_grouped = []
+        x2_grouped = []
 
         def quantise_x(r):
-            grouped = grouped_points[r][0][:].rearrange("p b n j -> p (b n j)")
-            return quantise(nc, points_mx_pool, grouped, COLS, "x")
+            grouped = x_grouped[r][:].rearrange("p b n j -> p (b n j)")
+            x_mx.append(quantise(nc, points_mx_pool, grouped, COLS, "x"))
 
         def quantise_x2(r):
-            grouped = grouped_points[r][1][:].rearrange("p b n j -> p (b n j)")
-            return quantise(nc, points_mx_pool, grouped, COLS, "x2")
+            grouped = x2_grouped[r][:].rearrange("p b n j -> p (b n j)")
+            x2_mx.append(quantise(nc, points_mx_pool, grouped, COLS, "x2"))
 
-        ctx.enter_context(tc.manual_schedule(engines={mybir.EngineType.DVE}))
-        x_mx = {0: quantise_x(0)}
-        x2_mx = {0: quantise_x2(0)}
+        x_mx = []
+        x2_mx = []
+        phi_w_grouped = turn_weights(phi_w_rows, (nc.vector.tensor_copy, nc.scalar.copy), "phi_w")
+        regroup_x2(0)
+        phi_w_mx = quantise(nc, const, phi_w_grouped[:], PACK * P, "phi_w")
+        phi_bias = widen_bias(phi_b_bf16, "phi_b")
+        quantise_x2(0)
+        theta_w_grouped = turn_weights(theta_w_rows, (nc.scalar.copy, nc.scalar.copy), "theta_w")
+        for b in range(ROUND_B):
+            regroup_x_batch(0, b)
+        regroup_x2(1)
+
         for r in range(ROUNDS):
             if r + LOAD_AHEAD < ROUNDS:
                 x2_raws.append(load_points(x_2, r + LOAD_AHEAD, "x2"))
@@ -219,23 +256,30 @@ def tile_sgcam_pa_t_kernel(tc, x, x_2, theta_w, theta_b, phi_w, phi_b, out):
             for i in range(VECTOR_TILES):
                 bank = project_tile(phi_w_mx, x2_mx[r], i)
                 vector_empties(bank, phi_bias, phi_grouped, i)
+            if r == 0:
+                for later in range(1, REGROUP_AHEAD):
+                    for b in range(ROUND_B):
+                        regroup_x_batch(later, b)
+                theta_w_mx = quantise(nc, const, theta_w_grouped[:], PACK * P, "theta_w")
+                theta_bias = widen_bias(theta_b_bf16, "theta_b")
+                quantise_x(0)
             for i in range(TILES):
+                if i == BATCH_TILES and r > 0:
+                    finish(r - 1, theta_mx, phi_mx, r + REGROUP_AHEAD - 1)
                 bank = project_tile(theta_w_mx, x_mx[r], i)
                 vector_empties(bank, theta_bias, theta_grouped, i)
 
-            if r + REGROUP_AHEAD < ROUNDS:
-                grouped_points.append(
-                    regroup_points(x_raws[r + REGROUP_AHEAD], x2_raws[r + REGROUP_AHEAD])
-                )
+            for later in range(len(x2_grouped), min(r + REGROUP_AHEAD + 1, ROUNDS)):
+                regroup_x2(later)
 
-            if r == 0:
-                x_mx[1] = quantise_x(1)
-                x2_mx[1] = quantise_x2(1)
-            ahead = r + QUANTISE_AHEAD
+            if r < QUANTISE_AHEAD:
+                quantise_x2(r + 1)
+                quantise_x(r + 1)
+            ahead = r + QUANTISE_AHEAD if r > 0 else ROUNDS
             phi_mx = quantise(nc, work, phi_grouped[:].rearrange("m c t -> m (c t)"), COLS, "phi")
             if ahead < ROUNDS:
-                x_mx[ahead] = quantise_x(ahead)
+                quantise_x(ahead)
             theta_mx = quantise(nc, work, theta_grouped[:].rearrange("m c t -> m (c t)"), COLS, "theta")
             if ahead < ROUNDS:
-                x2_mx[ahead] = quantise_x2(ahead)
-            affinity(r, theta_mx, phi_mx)
+                quantise_x2(ahead)
+        finish(ROUNDS - 1, theta_mx, phi_mx, ROUNDS)

@@ -144,6 +144,23 @@ def tile_sgcam_pa_t_kernel(tc, x, x_2, theta_w, theta_b, phi_w, phi_b, out):
                 )
             return bank
 
+        def project_pair(w_mx, points_mx, first, h):
+            w_codes, w_scales = w_mx
+            codes, scales = points_mx
+            bank = conv_psum.tile([P, 2, N], F32, tag="bank")
+            for u in range(2):
+                t = 2 * h + u
+                nc.tensor.matmul_mx(
+                    out=bank[:, u, :],
+                    lhsT=w_codes[:, t * P : (t + 1) * P].bitcast(FP8X4),
+                    lhsT_scale=w_scales[:, t * P : (t + 1) * P],
+                    rhs=codes[:, first : first + N].bitcast(FP8X4),
+                    rhs_scale=scales[:, first : first + N],
+                    start=True,
+                    stop=True,
+                )
+            return bank
+
         def vector_empties(bank, bias, grouped, i):
             nc.vector.tensor_tensor(
                 out=grouped[:, i * P : (i + 1) * P, :],
@@ -152,11 +169,12 @@ def tile_sgcam_pa_t_kernel(tc, x, x_2, theta_w, theta_b, phi_w, phi_b, out):
                 op=ADD,
             )
 
-        def scalar_empties(bank, bias, rows, i):
-            for t in range(PACK):
+        def scalar_empties(bank, bias, rows, h):
+            for u in range(2):
+                t = 2 * h + u
                 nc.scalar.activation(
-                    out=rows[:, t, i * P : (i + 1) * P],
-                    in_=bank[:, t, :],
+                    out=rows[:, t, :],
+                    in_=bank[:, u, :],
                     func=IDENTITY,
                     bias=bias[:, t : t + 1],
                     scale=1.0,
@@ -246,9 +264,9 @@ def tile_sgcam_pa_t_kernel(tc, x, x_2, theta_w, theta_b, phi_w, phi_b, out):
             theta_grouped = work.tile([P, COLS, PACK], BF16, name="theta_grouped", align_bytes=64)
             phi_grouped = work.tile([P, COLS, PACK], BF16, name="phi_grouped", align_bytes=64)
             phi_rows = work.tile([P, PACK, SCALAR_TILES * P], BF16, name="phi_rows")
-            for i in range(SCALAR_TILES):
-                bank = project_tile(phi_w_mx, x2_mx[r], VECTOR_TILES + i)
-                scalar_empties(bank, phi_bias, phi_rows, i)
+            for h in range(PACK // 2):
+                bank = project_pair(phi_w_mx, x2_mx[r], VECTOR_TILES * P, h)
+                scalar_empties(bank, phi_bias, phi_rows, h)
             nc.scalar.copy(
                 out=phi_grouped[:, VECTOR_TILES * P :, :].rearrange("m (c i) t -> m c t i", i=RUN),
                 in_=phi_rows[:].rearrange("m t (c i) -> m c t i", i=RUN),

@@ -48,9 +48,10 @@ def tile_sgcam_pa_t_kernel(tc, x, x_2, theta_w, theta_b, phi_w, phi_b, out):
         front = ctx.enter_context(tc.tile_pool(name="front", bufs=REGROUP_AHEAD + 1))
         x2_front = ctx.enter_context(tc.tile_pool(name="x2_front", bufs=2))
         points_mx_pool = ctx.enter_context(tc.tile_pool(name="points_mx", bufs=QUANTISE_AHEAD + 1))
-        work = ctx.enter_context(tc.tile_pool(name="work", bufs=2))
+        work = ctx.enter_context(tc.tile_pool(name="work", bufs=3))
         result_pool = ctx.enter_context(tc.tile_pool(name="result", bufs=3))
-        conv_psum = ctx.enter_context(tc.psum_pool(name="conv_psum", bufs=6))
+        conv_psum = ctx.enter_context(tc.psum_pool(name="conv_psum", bufs=4))
+        pair_psum = ctx.enter_context(tc.psum_pool(name="pair_psum", bufs=2))
         out_psum = ctx.enter_context(tc.psum_pool(name="out_psum", bufs=2))
 
         def load_points(src, r, name):
@@ -147,7 +148,7 @@ def tile_sgcam_pa_t_kernel(tc, x, x_2, theta_w, theta_b, phi_w, phi_b, out):
         def project_pair(w_mx, points_mx, first, h):
             w_codes, w_scales = w_mx
             codes, scales = points_mx
-            bank = conv_psum.tile([P, 2, N], F32, tag="bank")
+            bank = pair_psum.tile([P, 2, N], F32, name="pair")
             for u in range(2):
                 t = 2 * h + u
                 nc.tensor.matmul_mx(
@@ -256,21 +257,28 @@ def tile_sgcam_pa_t_kernel(tc, x, x_2, theta_w, theta_b, phi_w, phi_b, out):
             regroup_x_batch(0, b)
         regroup_x2(1)
 
+        def scalar_share(r):
+            grouped = work.tile([P, COLS, PACK], BF16, name="phi_grouped", align_bytes=64)
+            rows = work.tile([P, PACK, SCALAR_TILES * P], BF16, name="phi_rows")
+            for h in range(PACK // 2):
+                bank = project_pair(phi_w_mx, x2_mx[r], VECTOR_TILES * P, h)
+                scalar_empties(bank, phi_bias, rows, h)
+            nc.scalar.copy(
+                out=grouped[:, VECTOR_TILES * P :, :].rearrange("m (c i) t -> m c t i", i=RUN),
+                in_=rows[:].rearrange("m t (c i) -> m c t i", i=RUN),
+            )
+            phi_groups.append(grouped)
+
+        phi_groups = []
+        scalar_share(0)
+
         for r in range(ROUNDS):
             if r + LOAD_AHEAD < ROUNDS:
                 x2_raws.append(load_points(x_2, r + LOAD_AHEAD, "x2"))
                 x_raws.append(load_points(x, r + LOAD_AHEAD, "x"))
 
             theta_grouped = work.tile([P, COLS, PACK], BF16, name="theta_grouped", align_bytes=64)
-            phi_grouped = work.tile([P, COLS, PACK], BF16, name="phi_grouped", align_bytes=64)
-            phi_rows = work.tile([P, PACK, SCALAR_TILES * P], BF16, name="phi_rows")
-            for h in range(PACK // 2):
-                bank = project_pair(phi_w_mx, x2_mx[r], VECTOR_TILES * P, h)
-                scalar_empties(bank, phi_bias, phi_rows, h)
-            nc.scalar.copy(
-                out=phi_grouped[:, VECTOR_TILES * P :, :].rearrange("m (c i) t -> m c t i", i=RUN),
-                in_=phi_rows[:].rearrange("m t (c i) -> m c t i", i=RUN),
-            )
+            phi_grouped = phi_groups[r]
             for i in range(VECTOR_TILES):
                 bank = project_tile(phi_w_mx, x2_mx[r], i)
                 vector_empties(bank, phi_bias, phi_grouped, i)
@@ -287,12 +295,16 @@ def tile_sgcam_pa_t_kernel(tc, x, x_2, theta_w, theta_b, phi_w, phi_b, out):
                 bank = project_tile(theta_w_mx, x_mx[r], i)
                 vector_empties(bank, theta_bias, theta_grouped, i)
 
+            if QUANTISE_AHEAD <= r < ROUNDS - 1:
+                scalar_share(r + 1)
+
             for later in range(len(x2_grouped), min(r + REGROUP_AHEAD + 1, ROUNDS)):
                 regroup_x2(later)
 
             if r < QUANTISE_AHEAD:
                 quantise_x2(r + 1)
                 quantise_x(r + 1)
+                scalar_share(r + 1)
             ahead = r + QUANTISE_AHEAD if r > 0 else ROUNDS
             phi_mx = quantise(nc, work, phi_grouped[:].rearrange("m c t -> m (c t)"), COLS, "phi")
             if ahead < ROUNDS:

@@ -100,15 +100,40 @@ def tile_sgcam_pa_t_kernel(tc, x, x_2, theta_w, theta_b, phi_w, phi_b, out):
                 )
             return w_grouped
 
+        def gpsimd_regroup(grouped, raw):
+            nc.gpsimd.tensor_scalar(
+                out=grouped,
+                in0=raw.rearrange("p j n -> p n j"),
+                scalar1=1.0,
+                scalar2=0.0,
+                op0=MULT,
+                op1=ADD,
+            )
+
         def regroup_x_batch(r, b):
             if b == 0:
                 x_grouped.append(
                     front.tile([P, ROUND_B, N, PACK], BF16, name="x_grouped", align_bytes=64)
                 )
-            nc.scalar.copy(
-                out=x_grouped[r][:, b].rearrange("p (c i) j -> p c j i", i=RUN),
-                in_=x_raws[r][:, b].rearrange("p j (c i) -> p c j i", i=RUN),
-            )
+            if r == 0 and b == 1:
+                gpsimd_regroup(x_grouped[r][:, b], x_raws[r][:, b])
+            else:
+                nc.scalar.copy(
+                    out=x_grouped[r][:, b].rearrange("p (c i) j -> p c j i", i=RUN),
+                    in_=x_raws[r][:, b].rearrange("p j (c i) -> p c j i", i=RUN),
+                )
+
+        def turn_x_batch(r, b):
+            turned = pair_psum.tile([P, N, PACK], BF16, name="pair")
+            for i in range(BATCH_TILES):
+                nc.tensor.matmul(
+                    turned[:, i * P : (i + 1) * P, :],
+                    lhsT=ident_bf16[:],
+                    rhs=x_raws[r][:, b, :, i * P : (i + 1) * P].rearrange("p j n -> p n j"),
+                    start=True,
+                    stop=True,
+                )
+            return turned
 
         def regroup_x2(r):
             grouped = x2_front.tile([P, ROUND_B, N, PACK], BF16, name="x2_grouped", align_bytes=64)
@@ -119,20 +144,17 @@ def tile_sgcam_pa_t_kernel(tc, x, x_2, theta_w, theta_b, phi_w, phi_b, out):
                         in_=x2_raws[r][:, b].rearrange("p j (c i) -> p c j i", i=RUN),
                     )
                 else:
-                    nc.gpsimd.tensor_scalar(
-                        out=grouped[:, b],
-                        in0=x2_raws[r][:, b].rearrange("p j n -> p n j"),
-                        scalar1=1.0,
-                        scalar2=0.0,
-                        op0=MULT,
-                        op1=ADD,
-                    )
+                    gpsimd_regroup(grouped[:, b], x2_raws[r][:, b])
             x2_grouped.append(grouped)
 
         def project_tile(w_mx, points_mx, i):
+            bank = conv_psum.tile([P, PACK, P], F32, tag="bank")
+            project_into(bank, w_mx, points_mx, i)
+            return bank
+
+        def project_into(bank, w_mx, points_mx, i):
             w_codes, w_scales = w_mx
             codes, scales = points_mx
-            bank = conv_psum.tile([P, PACK, P], F32, tag="bank")
             for t in range(PACK):
                 nc.tensor.matmul_mx(
                     out=bank[:, t, :],
@@ -143,7 +165,6 @@ def tile_sgcam_pa_t_kernel(tc, x, x_2, theta_w, theta_b, phi_w, phi_b, out):
                     start=True,
                     stop=True,
                 )
-            return bank
 
         def project_pair(w_mx, points_mx, first, h):
             w_codes, w_scales = w_mx
@@ -181,25 +202,40 @@ def tile_sgcam_pa_t_kernel(tc, x, x_2, theta_w, theta_b, phi_w, phi_b, out):
                     scale=1.0,
                 )
 
-        def affinity(theta_mx, phi_mx):
+        def affinity_tile(product, theta_mx, first, phi_mx, b):
             theta_codes, theta_scales = theta_mx
             phi_codes, phi_scales = phi_mx
+            nc.tensor.matmul_mx(
+                out=product,
+                lhsT=theta_codes[:, first : first + P].bitcast(FP8X4),
+                lhsT_scale=theta_scales[:, first : first + P],
+                rhs=phi_codes[:, b * N : (b + 1) * N].bitcast(FP8X4),
+                rhs_scale=phi_scales[:, b * N : (b + 1) * N],
+                start=True,
+                stop=True,
+            )
+
+        def affinity(theta_mx, phi_mx):
             products = []
             for b in range(ROUND_B):
                 product = out_psum.tile([P, BATCH_TILES, N], F32, name="product")
                 for i in range(BATCH_TILES):
-                    first = b * N + i * P
-                    nc.tensor.matmul_mx(
-                        out=product[:, i, :],
-                        lhsT=theta_codes[:, first : first + P].bitcast(FP8X4),
-                        lhsT_scale=theta_scales[:, first : first + P],
-                        rhs=phi_codes[:, b * N : (b + 1) * N].bitcast(FP8X4),
-                        rhs_scale=phi_scales[:, b * N : (b + 1) * N],
-                        start=True,
-                        stop=True,
-                    )
+                    affinity_tile(product[:, i, :], theta_mx, b * N + i * P, phi_mx, b)
                 products.append(product)
             return products
+
+        def finish_tiles(b, theta_mx, phi_mx):
+            for i in range(BATCH_TILES):
+                product = out_psum.tile([P, N], F32, name="product")
+                affinity_tile(product[:], theta_mx, i * P, phi_mx, b)
+                result = result_pool.tile([P, N], F32, name="last_result")
+                if i == 0:
+                    nc.scalar.mul(out=result[:], in_=product[:], mul=1.0 / N)
+                else:
+                    nc.vector.tensor_scalar_mul(out=result[:], in0=product[:], scalar1=1.0 / N)
+                nc.sync.dma_start(
+                    out=out[(ROUNDS - 1) * ROUND_B + b, i * P : (i + 1) * P, :], in_=result[:]
+                )
 
         def store(r, result):
             nc.sync.dma_start(
@@ -208,11 +244,14 @@ def tile_sgcam_pa_t_kernel(tc, x, x_2, theta_w, theta_b, phi_w, phi_b, out):
             )
 
         def finish(r, theta_mx, phi_mx, x_round):
+            turned = turn_x_batch(x_round, 1) if x_round < ROUNDS else None
             products = affinity(theta_mx, phi_mx)
             result = result_pool.tile([P, ROUND_B, BATCH_TILES, N], F32, name="result")
             for b in range(ROUND_B):
-                if x_round < ROUNDS:
+                if b == 0 and x_round < ROUNDS:
                     regroup_x_batch(x_round, b)
+                elif x_round < ROUNDS:
+                    nc.scalar.copy(out=x_grouped[x_round][:, b], in_=turned[:])
                 nc.scalar.mul(out=result[:, b], in_=products[b][:], mul=1.0 / N)
             store(r, result)
 
@@ -234,6 +273,8 @@ def tile_sgcam_pa_t_kernel(tc, x, x_2, theta_w, theta_b, phi_w, phi_b, out):
 
         ident = const.tile([P, P], F32, name="ident")
         make_identity(nc, ident[:])
+        ident_bf16 = const.tile([P, P], BF16, name="ident_bf16")
+        nc.gpsimd.tensor_copy(out=ident_bf16[:], in_=ident[:])
         x_grouped = []
         x2_grouped = []
 
@@ -256,9 +297,11 @@ def tile_sgcam_pa_t_kernel(tc, x, x_2, theta_w, theta_b, phi_w, phi_b, out):
         for b in range(ROUND_B):
             regroup_x_batch(0, b)
         regroup_x2(1)
+        theta_w_mx = quantise(nc, const, theta_w_grouped[:], PACK * P, "theta_w")
+        theta_bias = widen_bias(theta_b_bf16, "theta_b")
 
         def scalar_share(r):
-            grouped = work.tile([P, COLS, PACK], BF16, name="phi_grouped", align_bytes=64)
+            grouped = phi_groups[r]
             rows = work.tile([P, PACK, SCALAR_TILES * P], BF16, name="phi_rows")
             for h in range(PACK // 2):
                 bank = project_pair(phi_w_mx, x2_mx[r], VECTOR_TILES * P, h)
@@ -267,10 +310,25 @@ def tile_sgcam_pa_t_kernel(tc, x, x_2, theta_w, theta_b, phi_w, phi_b, out):
                 out=grouped[:, VECTOR_TILES * P :, :].rearrange("m (c i) t -> m c t i", i=RUN),
                 in_=rows[:].rearrange("m t (c i) -> m c t i", i=RUN),
             )
-            phi_groups.append(grouped)
+
+        def scalar_tile(w_mx, points_mx, bias, grouped, i):
+            bank = pair_psum.tile([P, PACK, P], F32, name="pair")
+            project_into(bank, w_mx, points_mx, i)
+            rows = work.tile([P, PACK, P], BF16, name="tile_rows")
+            for t in range(PACK):
+                nc.scalar.activation(
+                    out=rows[:, t, :],
+                    in_=bank[:, t, :],
+                    func=IDENTITY,
+                    bias=bias[:, t : t + 1],
+                    scale=1.0,
+                )
+            nc.scalar.copy(
+                out=grouped[:, i * P : (i + 1) * P, :].rearrange("m (c i) t -> m c t i", i=RUN),
+                in_=rows[:].rearrange("m t (c i) -> m c t i", i=RUN),
+            )
 
         phi_groups = []
-        scalar_share(0)
 
         for r in range(ROUNDS):
             if r + LOAD_AHEAD < ROUNDS:
@@ -278,38 +336,55 @@ def tile_sgcam_pa_t_kernel(tc, x, x_2, theta_w, theta_b, phi_w, phi_b, out):
                 x_raws.append(load_points(x, r + LOAD_AHEAD, "x"))
 
             theta_grouped = work.tile([P, COLS, PACK], BF16, name="theta_grouped", align_bytes=64)
-            phi_grouped = phi_groups[r]
+            while len(phi_groups) < min(r + 2, ROUNDS):
+                phi_groups.append(
+                    work.tile([P, COLS, PACK], BF16, name="phi_grouped", align_bytes=64)
+                )
             for i in range(VECTOR_TILES):
+                if r == 0 and i == 1:
+                    quantise_x(0)
                 bank = project_tile(phi_w_mx, x2_mx[r], i)
-                vector_empties(bank, phi_bias, phi_grouped, i)
+                vector_empties(bank, phi_bias, phi_groups[r], i)
             if r == 0:
+                scalar_share(0)
                 for later in range(1, REGROUP_AHEAD):
                     for b in range(ROUND_B):
                         regroup_x_batch(later, b)
-                theta_w_mx = quantise(nc, const, theta_w_grouped[:], PACK * P, "theta_w")
-                theta_bias = widen_bias(theta_b_bf16, "theta_b")
-                quantise_x(0)
-            for i in range(TILES):
-                if i == BATCH_TILES and r > 0:
-                    finish(r - 1, theta_mx, phi_mx, r + REGROUP_AHEAD - 1)
+            last = r == ROUNDS - 1
+            scalar_theta = 1 if r >= ROUNDS - QUANTISE_AHEAD else 0
+            for i in range(BATCH_TILES):
                 bank = project_tile(theta_w_mx, x_mx[r], i)
                 vector_empties(bank, theta_bias, theta_grouped, i)
-
-            if QUANTISE_AHEAD <= r < ROUNDS - 1:
-                scalar_share(r + 1)
+            if r > 0:
+                finish(r - 1, theta_mx, phi_mx, r + REGROUP_AHEAD - 1)
+            phi_cols = phi_groups[r][:].rearrange("m c t -> m (c t)")
+            theta_cols = theta_grouped[:].rearrange("m c t -> m (c t)")
+            half = N * PACK
+            if scalar_theta:
+                scalar_tile(theta_w_mx, x_mx[r], theta_bias, theta_grouped, TILES - 1)
+            if last:
+                phi_mx = quantise(nc, work, phi_cols, COLS, "phi")
+                theta_first = quantise(nc, work, theta_cols[:, :half], N, "theta_first")
+            for i in range(BATCH_TILES, TILES - scalar_theta):
+                bank = project_tile(theta_w_mx, x_mx[r], i)
+                vector_empties(bank, theta_bias, theta_grouped, i)
+            if last:
+                theta_second = quantise(nc, work, theta_cols[:, half:], N, "theta_second")
+                finish_tiles(0, theta_first, phi_mx)
+                finish_tiles(1, theta_second, phi_mx)
+                break
 
             for later in range(len(x2_grouped), min(r + REGROUP_AHEAD + 1, ROUNDS)):
                 regroup_x2(later)
 
-            if r < QUANTISE_AHEAD:
+            if len(x2_mx) == r + 1 < ROUNDS:
                 quantise_x2(r + 1)
-                quantise_x(r + 1)
+            if r + 1 < ROUNDS:
                 scalar_share(r + 1)
-            ahead = r + QUANTISE_AHEAD if r > 0 else ROUNDS
-            phi_mx = quantise(nc, work, phi_grouped[:].rearrange("m c t -> m (c t)"), COLS, "phi")
-            if ahead < ROUNDS:
-                quantise_x(ahead)
-            theta_mx = quantise(nc, work, theta_grouped[:].rearrange("m c t -> m (c t)"), COLS, "theta")
-            if ahead < ROUNDS:
-                quantise_x2(ahead)
-        finish(ROUNDS - 1, theta_mx, phi_mx, ROUNDS)
+            phi_mx = quantise(nc, work, phi_cols, COLS, "phi")
+            quantised_to = min(r + QUANTISE_AHEAD if r > 0 else 1, ROUNDS - 1)
+            while len(x_mx) <= quantised_to:
+                quantise_x(len(x_mx))
+            theta_mx = quantise(nc, work, theta_cols, COLS, "theta")
+            while len(x2_mx) <= quantised_to:
+                quantise_x2(len(x2_mx))

@@ -26,7 +26,6 @@ TILES = COLS // P
 BATCH_TILES = N // P
 SCALAR_TILES = 2
 VECTOR_TILES = TILES - SCALAR_TILES
-REGROUP_AHEAD = 3
 QUANTISE_AHEAD = 2
 LOAD_AHEAD = 6
 
@@ -45,8 +44,8 @@ def tile_sgcam_pa_t_kernel(tc, x, x_2, theta_w, theta_b, phi_w, phi_b, out):
     with ExitStack() as ctx:
         const = ctx.enter_context(tc.tile_pool(name="const", bufs=1))
         raw_pool = ctx.enter_context(tc.tile_pool(name="raw", bufs=LOAD_AHEAD))
-        front = ctx.enter_context(tc.tile_pool(name="front", bufs=REGROUP_AHEAD + 1))
-        x2_front = ctx.enter_context(tc.tile_pool(name="x2_front", bufs=2))
+        front = ctx.enter_context(tc.tile_pool(name="front", bufs=3))
+        x2_front = ctx.enter_context(tc.tile_pool(name="x2_front", bufs=1))
         points_mx_pool = ctx.enter_context(tc.tile_pool(name="points_mx", bufs=QUANTISE_AHEAD + 1))
         work = ctx.enter_context(tc.tile_pool(name="work", bufs=3))
         result_pool = ctx.enter_context(tc.tile_pool(name="result", bufs=3))
@@ -110,42 +109,31 @@ def tile_sgcam_pa_t_kernel(tc, x, x_2, theta_w, theta_b, phi_w, phi_b, out):
                 op1=ADD,
             )
 
-        def regroup_x_batch(r, b):
-            if b == 0:
-                x_grouped.append(
-                    front.tile([P, ROUND_B, N, PACK], BF16, name="x_grouped", align_bytes=64)
-                )
-            if r == 0 and b == 1:
-                gpsimd_regroup(x_grouped[r][:, b], x_raws[r][:, b])
-            else:
-                nc.scalar.copy(
-                    out=x_grouped[r][:, b].rearrange("p (c i) j -> p c j i", i=RUN),
-                    in_=x_raws[r][:, b].rearrange("p j (c i) -> p c j i", i=RUN),
-                )
+        def strided_copy(copy, grouped, raw):
+            copy(
+                out=grouped.rearrange("p (c i) j -> p c j i", i=RUN),
+                in_=raw.rearrange("p j (c i) -> p c j i", i=RUN),
+            )
 
-        def turn_x_batch(r, b):
+        def identity_turn(raw):
             turned = pair_psum.tile([P, N, PACK], BF16, name="pair")
             for i in range(BATCH_TILES):
                 nc.tensor.matmul(
                     turned[:, i * P : (i + 1) * P, :],
                     lhsT=ident_bf16[:],
-                    rhs=x_raws[r][:, b, :, i * P : (i + 1) * P].rearrange("p j n -> p n j"),
+                    rhs=raw[:, :, i * P : (i + 1) * P].rearrange("p j n -> p n j"),
                     start=True,
                     stop=True,
                 )
             return turned
 
-        def regroup_x2(r):
-            grouped = x2_front.tile([P, ROUND_B, N, PACK], BF16, name="x2_grouped", align_bytes=64)
+        def new_points(pool, points, r, name):
+            points[r] = pool.tile([P, ROUND_B, N, PACK], BF16, name=name, align_bytes=64)
+
+        def gpsimd_x2(r):
+            new_points(x2_front, x2_grouped, r, "x2_grouped")
             for b in range(ROUND_B):
-                if r == 0 and b == 0:
-                    nc.vector.tensor_copy(
-                        out=grouped[:, b].rearrange("p (c i) j -> p c j i", i=RUN),
-                        in_=x2_raws[r][:, b].rearrange("p j (c i) -> p c j i", i=RUN),
-                    )
-                else:
-                    gpsimd_regroup(grouped[:, b], x2_raws[r][:, b])
-            x2_grouped.append(grouped)
+                gpsimd_regroup(x2_grouped[r][:, b], x2_raws[r][:, b])
 
         def project_tile(w_mx, points_mx, i):
             bank = conv_psum.tile([P, PACK, P], F32, tag="bank")
@@ -244,17 +232,18 @@ def tile_sgcam_pa_t_kernel(tc, x, x_2, theta_w, theta_b, phi_w, phi_b, out):
             )
 
         def finish(r, theta_mx, phi_mx, x_round):
-            turned = turn_x_batch(x_round, 1) if x_round < ROUNDS else None
+            if x_round < ROUNDS:
+                new_points(front, x_grouped, x_round, "x_grouped")
+                turned = identity_turn(x_raws[x_round][:, 1])
             products = affinity(theta_mx, phi_mx)
             result = result_pool.tile([P, ROUND_B, BATCH_TILES, N], F32, name="result")
             for b in range(ROUND_B):
-                if b == 0 and x_round < ROUNDS:
-                    regroup_x_batch(x_round, b)
+                if x_round < ROUNDS and b == 0:
+                    strided_copy(nc.scalar.copy, x_grouped[x_round][:, b], x_raws[x_round][:, b])
                 elif x_round < ROUNDS:
                     nc.scalar.copy(out=x_grouped[x_round][:, b], in_=turned[:])
                 nc.scalar.mul(out=result[:, b], in_=products[b][:], mul=1.0 / N)
             store(r, result)
-
 
         ctx.enter_context(
             tc.manual_schedule(
@@ -275,28 +264,30 @@ def tile_sgcam_pa_t_kernel(tc, x, x_2, theta_w, theta_b, phi_w, phi_b, out):
         make_identity(nc, ident[:])
         ident_bf16 = const.tile([P, P], BF16, name="ident_bf16")
         nc.gpsimd.tensor_copy(out=ident_bf16[:], in_=ident[:])
-        x_grouped = []
-        x2_grouped = []
+        x_grouped = {}
+        x2_grouped = {}
+        x_mx = {}
+        x2_mx = {}
 
         def quantise_x(r):
             grouped = x_grouped[r][:].rearrange("p b n j -> p (b n j)")
-            x_mx.append(quantise(nc, points_mx_pool, grouped, COLS, "x"))
+            x_mx[r] = quantise(nc, points_mx_pool, grouped, COLS, "x")
 
         def quantise_x2(r):
             grouped = x2_grouped[r][:].rearrange("p b n j -> p (b n j)")
-            x2_mx.append(quantise(nc, points_mx_pool, grouped, COLS, "x2"))
+            x2_mx[r] = quantise(nc, points_mx_pool, grouped, COLS, "x2")
 
-        x_mx = []
-        x2_mx = []
         phi_w_grouped = turn_weights(phi_w_rows, (nc.vector.tensor_copy, nc.scalar.copy), "phi_w")
-        regroup_x2(0)
+        new_points(front, x2_grouped, 0, "x2_first")
+        for b in range(ROUND_B):
+            strided_copy(nc.vector.tensor_copy, x2_grouped[0][:, b], x2_raws[0][:, b])
         phi_w_mx = quantise(nc, const, phi_w_grouped[:], PACK * P, "phi_w")
         phi_bias = widen_bias(phi_b_bf16, "phi_b")
         quantise_x2(0)
         theta_w_grouped = turn_weights(theta_w_rows, (nc.scalar.copy, nc.scalar.copy), "theta_w")
-        for b in range(ROUND_B):
-            regroup_x_batch(0, b)
-        regroup_x2(1)
+        new_points(x2_front, x_grouped, 0, "x2_grouped")
+        strided_copy(nc.scalar.copy, x_grouped[0][:, 0], x_raws[0][:, 0])
+        strided_copy(nc.vector.tensor_copy, x_grouped[0][:, 1], x_raws[0][:, 1])
         theta_w_mx = quantise(nc, const, theta_w_grouped[:], PACK * P, "theta_w")
         theta_bias = widen_bias(theta_b_bf16, "theta_b")
 
@@ -329,62 +320,103 @@ def tile_sgcam_pa_t_kernel(tc, x, x_2, theta_w, theta_b, phi_w, phi_b, out):
             )
 
         phi_groups = []
+        theta_groups = []
+
+        def vector_phi(r, i):
+            vector_empties(project_tile(phi_w_mx, x2_mx[r], i), phi_bias, phi_groups[r], i)
+
+        def vector_theta(r, i):
+            vector_empties(project_tile(theta_w_mx, x_mx[r], i), theta_bias, theta_groups[r], i)
+
+        def quantise_phi(r):
+            return quantise(nc, work, phi_groups[r][:].rearrange("m c t -> m (c t)"), COLS, "phi")
+
+        def quantise_theta(r):
+            return quantise(
+                nc, work, theta_groups[r][:].rearrange("m c t -> m (c t)"), COLS, "theta"
+            )
+
+        def scalar_theta(r):
+            return 1 if r >= ROUNDS - QUANTISE_AHEAD else 0
 
         for r in range(ROUNDS):
+            last = r == ROUNDS - 1
             if r + LOAD_AHEAD < ROUNDS:
                 x2_raws.append(load_points(x_2, r + LOAD_AHEAD, "x2"))
                 x_raws.append(load_points(x, r + LOAD_AHEAD, "x"))
-
-            theta_grouped = work.tile([P, COLS, PACK], BF16, name="theta_grouped", align_bytes=64)
-            while len(phi_groups) < min(r + 2, ROUNDS):
+            while len(theta_groups) < min(r + 2, ROUNDS):
+                theta_groups.append(
+                    work.tile([P, COLS, PACK], BF16, name="theta_grouped", align_bytes=64)
+                )
                 phi_groups.append(
                     work.tile([P, COLS, PACK], BF16, name="phi_grouped", align_bytes=64)
                 )
-            for i in range(VECTOR_TILES):
-                if r == 0 and i == 1:
-                    quantise_x(0)
-                bank = project_tile(phi_w_mx, x2_mx[r], i)
-                vector_empties(bank, phi_bias, phi_groups[r], i)
+
             if r == 0:
+                vector_phi(0, 0)
+                quantise_x(0)
+                vector_phi(0, 1)
+                new_points(front, x_grouped, 1, "x_grouped")
+                for b in range(ROUND_B):
+                    strided_copy(nc.scalar.copy, x_grouped[1][:, b], x_raws[1][:, b])
                 scalar_share(0)
-                for later in range(1, REGROUP_AHEAD):
+                gpsimd_x2(1)
+                for i in range(TILES):
+                    vector_theta(0, i)
+                new_points(front, x_grouped, 2, "x_grouped")
+                new_points(front, x2_grouped, 2, "x2_first")
+                for grouped, raw in ((x_grouped[2], x_raws[2]), (x2_grouped[2], x2_raws[2])):
                     for b in range(ROUND_B):
-                        regroup_x_batch(later, b)
-            last = r == ROUNDS - 1
-            scalar_theta = 1 if r >= ROUNDS - QUANTISE_AHEAD else 0
+                        turned = identity_turn(raw[:, b])
+                        nc.scalar.copy(out=grouped[:, b], in_=turned[:])
+                quantise_x(1)
+                phi_mx = quantise_phi(0)
+                theta_mx = quantise_theta(0)
+                quantise_x2(1)
+                continue
+            if r == 1:
+                gpsimd_x2(3)
+                for i in range(TILES):
+                    vector_theta(1, i)
+                scalar_share(1)
+                for i in range(VECTOR_TILES):
+                    vector_phi(1, i)
+                finish(0, theta_mx, phi_mx, 3)
+                quantise_x2(2)
+                quantise_x(2)
+                scalar_share(2)
+                theta_mx = quantise_theta(1)
+                quantise_x(3)
+                phi_mx = quantise_phi(1)
+                quantise_x2(3)
+                continue
+
+            ahead = r + QUANTISE_AHEAD
+            if ahead < ROUNDS:
+                gpsimd_x2(ahead)
+            for i in range(VECTOR_TILES):
+                vector_phi(r, i)
             for i in range(BATCH_TILES):
-                bank = project_tile(theta_w_mx, x_mx[r], i)
-                vector_empties(bank, theta_bias, theta_grouped, i)
-            if r > 0:
-                finish(r - 1, theta_mx, phi_mx, r + REGROUP_AHEAD - 1)
-            phi_cols = phi_groups[r][:].rearrange("m c t -> m (c t)")
-            theta_cols = theta_grouped[:].rearrange("m c t -> m (c t)")
-            half = N * PACK
-            if scalar_theta:
-                scalar_tile(theta_w_mx, x_mx[r], theta_bias, theta_grouped, TILES - 1)
+                vector_theta(r, i)
+            finish(r - 1, theta_mx, phi_mx, ahead)
             if last:
-                phi_mx = quantise(nc, work, phi_cols, COLS, "phi")
+                theta_cols = theta_groups[r][:].rearrange("m c t -> m (c t)")
+                half = N * PACK
+                phi_mx = quantise_phi(r)
                 theta_first = quantise(nc, work, theta_cols[:, :half], N, "theta_first")
-            for i in range(BATCH_TILES, TILES - scalar_theta):
-                bank = project_tile(theta_w_mx, x_mx[r], i)
-                vector_empties(bank, theta_bias, theta_grouped, i)
+            for i in range(BATCH_TILES, TILES - scalar_theta(r)):
+                vector_theta(r, i)
             if last:
                 theta_second = quantise(nc, work, theta_cols[:, half:], N, "theta_second")
                 finish_tiles(0, theta_first, phi_mx)
                 finish_tiles(1, theta_second, phi_mx)
                 break
-
-            for later in range(len(x2_grouped), min(r + REGROUP_AHEAD + 1, ROUNDS)):
-                regroup_x2(later)
-
-            if len(x2_mx) == r + 1 < ROUNDS:
-                quantise_x2(r + 1)
-            if r + 1 < ROUNDS:
-                scalar_share(r + 1)
-            phi_mx = quantise(nc, work, phi_cols, COLS, "phi")
-            quantised_to = min(r + QUANTISE_AHEAD if r > 0 else 1, ROUNDS - 1)
-            while len(x_mx) <= quantised_to:
-                quantise_x(len(x_mx))
-            theta_mx = quantise(nc, work, theta_cols, COLS, "theta")
-            while len(x2_mx) <= quantised_to:
-                quantise_x2(len(x2_mx))
+            scalar_share(r + 1)
+            if scalar_theta(r + 1):
+                scalar_tile(theta_w_mx, x_mx[r + 1], theta_bias, theta_groups[r + 1], TILES - 1)
+            phi_mx = quantise_phi(r)
+            if ahead < ROUNDS:
+                quantise_x(ahead)
+            theta_mx = quantise_theta(r)
+            if ahead < ROUNDS:
+                quantise_x2(ahead)

@@ -67,7 +67,10 @@ def tile_sgcam_pa_t_kernel(tc, x, x_2, theta_w, theta_b, phi_w, phi_b, out):
 
         def load_weights(w, name):
             w_rows = const.tile([P, PACK, C], BF16, name=name + "_rows")
-            nc.sync.dma_start(out=w_rows[:], in_=w.rearrange("(m t) c -> m t c", t=PACK))
+            rows = w.rearrange("(m t) c -> m t c", t=PACK)
+            for half in range(2):
+                pair = slice(2 * half, 2 * half + 2)
+                nc.sync.dma_start(out=w_rows[:, pair], in_=rows[:, pair])
             return w_rows
 
         def load_bias(b, name):
@@ -364,11 +367,11 @@ def tile_sgcam_pa_t_kernel(tc, x, x_2, theta_w, theta_b, phi_w, phi_b, out):
                 for i in range(TILES):
                     vector_theta(0, i)
                 new_points(front, x_grouped, 2, "x_grouped")
+                for b in range(ROUND_B):
+                    strided_copy(nc.scalar.copy, x_grouped[2][:, b], x_raws[2][:, b])
                 new_points(front, x2_grouped, 2, "x2_first")
-                for grouped, raw in ((x_grouped[2], x_raws[2]), (x2_grouped[2], x2_raws[2])):
-                    for b in range(ROUND_B):
-                        turned = identity_turn(raw[:, b])
-                        nc.scalar.copy(out=grouped[:, b], in_=turned[:])
+                strided_copy(nc.scalar.copy, x2_grouped[2][:, 0], x2_raws[2][:, 0])
+                strided_copy(nc.vector.tensor_copy, x2_grouped[2][:, 1], x2_raws[2][:, 1])
                 quantise_x(1)
                 phi_mx = quantise_phi(0)
                 theta_mx = quantise_theta(0)

@@ -234,17 +234,25 @@ def tile_sgcam_pa_t_kernel(tc, x, x_2, theta_w, theta_b, phi_w, phi_b, out):
                 in_=result[:].rearrange("p b i m -> p (b i) m"),
             )
 
+        pending = []
+
+        def regroup_share():
+            if pending:
+                grouped, rows = pending.pop()
+                strided_copy(nc.scalar.copy, grouped[:, VECTOR_TILES * P :, :], rows[:])
+
         def finish(r, theta_mx, phi_mx, x_round):
             if x_round < ROUNDS:
                 new_points(front, x_grouped, x_round, "x_grouped")
                 turned = identity_turn(x_raws[x_round][:, 1])
             products = affinity(theta_mx, phi_mx)
             result = result_pool.tile([P, ROUND_B, BATCH_TILES, N], F32, name="result")
+            if x_round < ROUNDS:
+                strided_copy(nc.scalar.copy, x_grouped[x_round][:, 0], x_raws[x_round][:, 0])
+                regroup_share()
+                nc.scalar.copy(out=x_grouped[x_round][:, 1], in_=turned[:])
+            regroup_share()
             for b in range(ROUND_B):
-                if x_round < ROUNDS and b == 0:
-                    strided_copy(nc.scalar.copy, x_grouped[x_round][:, b], x_raws[x_round][:, b])
-                elif x_round < ROUNDS:
-                    nc.scalar.copy(out=x_grouped[x_round][:, b], in_=turned[:])
                 nc.scalar.mul(out=result[:, b], in_=products[b][:], mul=1.0 / N)
             store(r, result)
 
@@ -300,10 +308,9 @@ def tile_sgcam_pa_t_kernel(tc, x, x_2, theta_w, theta_b, phi_w, phi_b, out):
             for h in range(PACK // 2):
                 bank = project_pair(phi_w_mx, x2_mx[r], VECTOR_TILES * P, h)
                 scalar_empties(bank, phi_bias, rows, h)
-            nc.scalar.copy(
-                out=grouped[:, VECTOR_TILES * P :, :].rearrange("m (c i) t -> m c t i", i=RUN),
-                in_=rows[:].rearrange("m t (c i) -> m c t i", i=RUN),
-            )
+            pending.append((grouped, rows))
+            if r < QUANTISE_AHEAD:
+                regroup_share()
 
         def scalar_tile(w_mx, points_mx, bias, grouped, i):
             bank = pair_psum.tile([P, PACK, P], F32, name="pair")
@@ -385,12 +392,12 @@ def tile_sgcam_pa_t_kernel(tc, x, x_2, theta_w, theta_b, phi_w, phi_b, out):
                 for i in range(VECTOR_TILES):
                     vector_phi(1, i)
                 finish(0, theta_mx, phi_mx, 3)
-                quantise_x2(2)
                 quantise_x(2)
+                quantise_x2(2)
                 scalar_share(2)
                 theta_mx = quantise_theta(1)
-                quantise_x(3)
                 phi_mx = quantise_phi(1)
+                quantise_x(3)
                 quantise_x2(3)
                 continue
 

from contextlib import ExitStack

import concourse.mybir as mybir
from concourse.masks import make_identity

BF16 = mybir.dt.bfloat16
F32 = mybir.dt.float32
U32 = mybir.dt.uint32
U8 = mybir.dt.uint8
FP8X4 = mybir.dt.float8_e4m3fn_x4
IDENTITY = mybir.ActivationFunctionType.Identity
ADD = mybir.AluOpType.add
MULT = mybir.AluOpType.mult

B = 32
C = 512
CI = 512
N = 256
P = 128
PACK = 4
RUN = 4
ROUND_B = 2
COLS = ROUND_B * N
ROUNDS = B // ROUND_B
TILES = COLS // P
BATCH_TILES = N // P
SCALAR_TILES = 2
VECTOR_TILES = TILES - SCALAR_TILES
QUANTISE_AHEAD = 2
LOAD_AHEAD = 6

FLOPS = 2 * B * (2 * CI * C * N + N * N * CI)


def quantise(nc, pool, grouped, cols, name):
    codes = pool.tile([P, cols], U32, name=name + "_codes", align_bytes=64)
    scales = pool.tile([P, cols], U8, name=name + "_scales", align_bytes=64)
    nc.vector.quantize_mx(out=codes[:].bitcast(FP8X4), scales=scales[:], in_=grouped)
    return codes, scales


def tile_sgcam_pa_t_kernel(tc, x, x_2, theta_w, theta_b, phi_w, phi_b, out):
    nc = tc.nc
    with ExitStack() as ctx:
        const = ctx.enter_context(tc.tile_pool(name="const", bufs=1))
        raw_pool = ctx.enter_context(tc.tile_pool(name="raw", bufs=LOAD_AHEAD))
        front = ctx.enter_context(tc.tile_pool(name="front", bufs=3))
        x2_front = ctx.enter_context(tc.tile_pool(name="x2_front", bufs=1))
        points_mx_pool = ctx.enter_context(tc.tile_pool(name="points_mx", bufs=QUANTISE_AHEAD + 1))
        work = ctx.enter_context(tc.tile_pool(name="work", bufs=3))
        result_pool = ctx.enter_context(tc.tile_pool(name="result", bufs=3))
        conv_psum = ctx.enter_context(tc.psum_pool(name="conv_psum", bufs=4))
        pair_psum = ctx.enter_context(tc.psum_pool(name="pair_psum", bufs=2))
        out_psum = ctx.enter_context(tc.psum_pool(name="out_psum", bufs=2))

        def load_points(src, r, name):
            raw = raw_pool.tile([P, ROUND_B, PACK, N], BF16, name=name + "_raw")
            step = 1 if r == 0 else ROUND_B
            for b in range(0, ROUND_B, step):
                nc.sync.dma_start(
                    out=raw[:, b : b + step].rearrange("p b j n -> p b (j n)"),
                    in_=src[r * ROUND_B + b : r * ROUND_B + b + step].rearrange(
                        "b (p j) n -> p b (j n)", j=PACK
                    ),
                )
            return raw

        def load_weights(w, name):
            w_rows = const.tile([P, PACK, C], BF16, name=name + "_rows")
            rows = w.rearrange("(m t) c -> m t c", t=PACK)
            for half in range(2):
                pair = slice(2 * half, 2 * half + 2)
                nc.sync.dma_start(out=w_rows[:, pair], in_=rows[:, pair])
            return w_rows

        def load_bias(b, name):
            b_bf16 = const.tile([P, PACK], BF16, name=name + "_bf16")
            nc.scalar.dma_start(out=b_bf16[:], in_=b.rearrange("(m t) -> m t", t=PACK))
            return b_bf16

        def widen_bias(b_bf16, name):
            bias = const.tile([P, PACK], F32, name=name + "_f32")
            nc.vector.tensor_copy(out=bias[:], in_=b_bf16[:])
            return bias

        def turn_weights(w_rows, copies, name):
            w_grouped = const.tile([P, PACK * P * PACK], BF16, name=name + "_grouped", align_bytes=64)
            grouped_words = w_grouped[:].bitcast(F32).rearrange(
                "q (t m u) -> q t m u", t=PACK, u=2
            )
            for half in range(2):
                turned = conv_psum.tile([P, 2, 2, P], F32, tag="bank")
                for t2 in range(2):
                    words = w_rows[:, 2 * half + t2, :].bitcast(F32).rearrange(
                        "m (q u) -> m u q", u=2
                    )
                    for u in range(2):
                        nc.tensor.transpose(turned[:, t2, u, :], words[:, u, :], ident[:])
                copies[half](
                    out=grouped_words[:, 2 * half : 2 * half + 2],
                    in_=turned[:].rearrange("q t u m -> q t m u"),
                )
            return w_grouped

        def gpsimd_regroup(grouped, raw):
            nc.gpsimd.tensor_scalar(
                out=grouped,
                in0=raw.rearrange("p j n -> p n j"),
                scalar1=1.0,
                scalar2=0.0,
                op0=MULT,
                op1=ADD,
            )

        def strided_copy(copy, grouped, raw):
            copy(
                out=grouped.rearrange("p (c i) j -> p c j i", i=RUN),
                in_=raw.rearrange("p j (c i) -> p c j i", i=RUN),
            )

        def identity_turn(raw):
            turned = pair_psum.tile([P, N, PACK], BF16, name="pair")
            for i in range(BATCH_TILES):
                nc.tensor.matmul(
                    turned[:, i * P : (i + 1) * P, :],
                    lhsT=ident_bf16[:],
                    rhs=raw[:, :, i * P : (i + 1) * P].rearrange("p j n -> p n j"),
                    start=True,
                    stop=True,
                )
            return turned

        def new_points(pool, points, r, name):
            points[r] = pool.tile([P, ROUND_B, N, PACK], BF16, name=name, align_bytes=64)

        def gpsimd_x2(r):
            new_points(x2_front, x2_grouped, r, "x2_grouped")
            for b in range(ROUND_B):
                gpsimd_regroup(x2_grouped[r][:, b], x2_raws[r][:, b])

        def project_tile(w_mx, points_mx, i):
            bank = conv_psum.tile([P, PACK, P], F32, tag="bank")
            project_into(bank, w_mx, points_mx, i)
            return bank

        def project_into(bank, w_mx, points_mx, i):
            w_codes, w_scales = w_mx
            codes, scales = points_mx
            for t in range(PACK):
                nc.tensor.matmul_mx(
                    out=bank[:, t, :],
                    lhsT=w_codes[:, t * P : (t + 1) * P].bitcast(FP8X4),
                    lhsT_scale=w_scales[:, t * P : (t + 1) * P],
                    rhs=codes[:, i * P : (i + 1) * P].bitcast(FP8X4),
                    rhs_scale=scales[:, i * P : (i + 1) * P],
                    start=True,
                    stop=True,
                )

        def project_pair(w_mx, points_mx, first, h):
            w_codes, w_scales = w_mx
            codes, scales = points_mx
            bank = pair_psum.tile([P, 2, N], F32, name="pair")
            for u in range(2):
                t = 2 * h + u
                nc.tensor.matmul_mx(
                    out=bank[:, u, :],
                    lhsT=w_codes[:, t * P : (t + 1) * P].bitcast(FP8X4),
                    lhsT_scale=w_scales[:, t * P : (t + 1) * P],
                    rhs=codes[:, first : first + N].bitcast(FP8X4),
                    rhs_scale=scales[:, first : first + N],
                    start=True,
                    stop=True,
                )
            return bank

        def vector_empties(bank, bias, grouped, i):
            nc.vector.tensor_tensor(
                out=grouped[:, i * P : (i + 1) * P, :],
                in0=bank[:].rearrange("m t n -> m n t"),
                in1=bias[:].unsqueeze(1).to_broadcast([P, P, PACK]),
                op=ADD,
            )

        def scalar_empties(bank, bias, rows, h):
            for u in range(2):
                t = 2 * h + u
                nc.scalar.activation(
                    out=rows[:, t, :],
                    in_=bank[:, u, :],
                    func=IDENTITY,
                    bias=bias[:, t : t + 1],
                    scale=1.0,
                )

        def affinity_tile(product, theta_mx, first, phi_mx, b):
            theta_codes, theta_scales = theta_mx
            phi_codes, phi_scales = phi_mx
            nc.tensor.matmul_mx(
                out=product,
                lhsT=theta_codes[:, first : first + P].bitcast(FP8X4),
                lhsT_scale=theta_scales[:, first : first + P],
                rhs=phi_codes[:, b * N : (b + 1) * N].bitcast(FP8X4),
                rhs_scale=phi_scales[:, b * N : (b + 1) * N],
                start=True,
                stop=True,
            )

        def affinity(theta_mx, phi_mx):
            products = []
            for b in range(ROUND_B):
                product = out_psum.tile([P, BATCH_TILES, N], F32, name="product")
                for i in range(BATCH_TILES):
                    affinity_tile(product[:, i, :], theta_mx, b * N + i * P, phi_mx, b)
                products.append(product)
            return products

        def finish_tiles(b, theta_mx, phi_mx):
            for i in range(BATCH_TILES):
                product = out_psum.tile([P, N], F32, name="product")
                affinity_tile(product[:], theta_mx, i * P, phi_mx, b)
                result = result_pool.tile([P, N], F32, name="last_result")
                if i == 0:
                    nc.scalar.mul(out=result[:], in_=product[:], mul=1.0 / N)
                else:
                    nc.vector.tensor_scalar_mul(out=result[:], in0=product[:], scalar1=1.0 / N)
                nc.sync.dma_start(
                    out=out[(ROUNDS - 1) * ROUND_B + b, i * P : (i + 1) * P, :], in_=result[:]
                )

        def store(r, result):
            nc.sync.dma_start(
                out=out[r * ROUND_B : (r + 1) * ROUND_B].rearrange("b (i p) m -> p (b i) m", p=P),
                in_=result[:].rearrange("p b i m -> p (b i) m"),
            )

        pending = []

        def regroup_share():
            if pending:
                grouped, rows = pending.pop()
                strided_copy(nc.scalar.copy, grouped[:, VECTOR_TILES * P :, :], rows[:])

        def finish(r, theta_mx, phi_mx, x_round):
            if x_round < ROUNDS:
                new_points(front, x_grouped, x_round, "x_grouped")
                turned = identity_turn(x_raws[x_round][:, 1])
            products = affinity(theta_mx, phi_mx)
            result = result_pool.tile([P, ROUND_B, BATCH_TILES, N], F32, name="result")
            if x_round < ROUNDS:
                strided_copy(nc.scalar.copy, x_grouped[x_round][:, 0], x_raws[x_round][:, 0])
                regroup_share()
                nc.scalar.copy(out=x_grouped[x_round][:, 1], in_=turned[:])
            regroup_share()
            for b in range(ROUND_B):
                nc.scalar.mul(out=result[:, b], in_=products[b][:], mul=1.0 / N)
            store(r, result)

        ctx.enter_context(
            tc.manual_schedule(
                engines={mybir.EngineType.DVE, mybir.EngineType.Activation, mybir.EngineType.PE}
            )
        )
        phi_b_bf16 = load_bias(phi_b, "phi_b")
        theta_b_bf16 = load_bias(theta_b, "theta_b")
        phi_w_rows = load_weights(phi_w, "phi_w")
        x2_raws = [load_points(x_2, 0, "x2")]
        theta_w_rows = load_weights(theta_w, "theta_w")
        x_raws = [load_points(x, 0, "x")]
        for r in range(1, LOAD_AHEAD):
            x2_raws.append(load_points(x_2, r, "x2"))
            x_raws.append(load_points(x, r, "x"))

        ident = const.tile([P, P], F32, name="ident")
        make_identity(nc, ident[:])
        ident_bf16 = const.tile([P, P], BF16, name="ident_bf16")
        nc.gpsimd.tensor_copy(out=ident_bf16[:], in_=ident[:])
        x_grouped = {}
        x2_grouped = {}
        x_mx = {}
        x2_mx = {}

        def quantise_x(r):
            grouped = x_grouped[r][:].rearrange("p b n j -> p (b n j)")
            x_mx[r] = quantise(nc, points_mx_pool, grouped, COLS, "x")

        def quantise_x2(r):
            grouped = x2_grouped[r][:].rearrange("p b n j -> p (b n j)")
            x2_mx[r] = quantise(nc, points_mx_pool, grouped, COLS, "x2")

        phi_w_grouped = turn_weights(phi_w_rows, (nc.vector.tensor_copy, nc.scalar.copy), "phi_w")
        new_points(front, x2_grouped, 0, "x2_first")
        for b in range(ROUND_B):
            strided_copy(nc.vector.tensor_copy, x2_grouped[0][:, b], x2_raws[0][:, b])
        phi_w_mx = quantise(nc, const, phi_w_grouped[:], PACK * P, "phi_w")
        phi_bias = widen_bias(phi_b_bf16, "phi_b")
        quantise_x2(0)
        theta_w_grouped = turn_weights(theta_w_rows, (nc.scalar.copy, nc.scalar.copy), "theta_w")
        new_points(x2_front, x_grouped, 0, "x2_grouped")
        strided_copy(nc.scalar.copy, x_grouped[0][:, 0], x_raws[0][:, 0])
        strided_copy(nc.vector.tensor_copy, x_grouped[0][:, 1], x_raws[0][:, 1])
        theta_w_mx = quantise(nc, const, theta_w_grouped[:], PACK * P, "theta_w")
        theta_bias = widen_bias(theta_b_bf16, "theta_b")

        def scalar_share(r):
            grouped = phi_groups[r]
            rows = work.tile([P, PACK, SCALAR_TILES * P], BF16, name="phi_rows")
            for h in range(PACK // 2):
                bank = project_pair(phi_w_mx, x2_mx[r], VECTOR_TILES * P, h)
                scalar_empties(bank, phi_bias, rows, h)
            pending.append((grouped, rows))
            if r < QUANTISE_AHEAD:
                regroup_share()

        def scalar_tile(w_mx, points_mx, bias, grouped, i):
            bank = pair_psum.tile([P, PACK, P], F32, name="pair")
            project_into(bank, w_mx, points_mx, i)
            rows = work.tile([P, PACK, P], BF16, name="tile_rows")
            for t in range(PACK):
                nc.scalar.activation(
                    out=rows[:, t, :],
                    in_=bank[:, t, :],
                    func=IDENTITY,
                    bias=bias[:, t : t + 1],
                    scale=1.0,
                )
            nc.scalar.copy(
                out=grouped[:, i * P : (i + 1) * P, :].rearrange("m (c i) t -> m c t i", i=RUN),
                in_=rows[:].rearrange("m t (c i) -> m c t i", i=RUN),
            )

        phi_groups = []
        theta_groups = []

        def vector_phi(r, i):
            vector_empties(project_tile(phi_w_mx, x2_mx[r], i), phi_bias, phi_groups[r], i)

        def vector_theta(r, i):
            vector_empties(project_tile(theta_w_mx, x_mx[r], i), theta_bias, theta_groups[r], i)

        def quantise_phi(r):
            return quantise(nc, work, phi_groups[r][:].rearrange("m c t -> m (c t)"), COLS, "phi")

        def quantise_theta(r):
            return quantise(
                nc, work, theta_groups[r][:].rearrange("m c t -> m (c t)"), COLS, "theta"
            )

        def scalar_theta(r):
            return 1 if r >= ROUNDS - QUANTISE_AHEAD else 0

        for r in range(ROUNDS):
            last = r == ROUNDS - 1
            if r + LOAD_AHEAD < ROUNDS:
                x2_raws.append(load_points(x_2, r + LOAD_AHEAD, "x2"))
                x_raws.append(load_points(x, r + LOAD_AHEAD, "x"))
            while len(theta_groups) < min(r + 2, ROUNDS):
                theta_groups.append(
                    work.tile([P, COLS, PACK], BF16, name="theta_grouped", align_bytes=64)
                )
                phi_groups.append(
                    work.tile([P, COLS, PACK], BF16, name="phi_grouped", align_bytes=64)
                )

            if r == 0:
                vector_phi(0, 0)
                quantise_x(0)
                vector_phi(0, 1)
                new_points(front, x_grouped, 1, "x_grouped")
                for b in range(ROUND_B):
                    strided_copy(nc.scalar.copy, x_grouped[1][:, b], x_raws[1][:, b])
                scalar_share(0)
                gpsimd_x2(1)
                for i in range(TILES):
                    vector_theta(0, i)
                new_points(front, x_grouped, 2, "x_grouped")
                for b in range(ROUND_B):
                    strided_copy(nc.scalar.copy, x_grouped[2][:, b], x_raws[2][:, b])
                new_points(front, x2_grouped, 2, "x2_first")
                strided_copy(nc.scalar.copy, x2_grouped[2][:, 0], x2_raws[2][:, 0])
                strided_copy(nc.vector.tensor_copy, x2_grouped[2][:, 1], x2_raws[2][:, 1])
                quantise_x(1)
                phi_mx = quantise_phi(0)
                theta_mx = quantise_theta(0)
                quantise_x2(1)
                continue
            if r == 1:
                gpsimd_x2(3)
                for i in range(TILES):
                    vector_theta(1, i)
                scalar_share(1)
                for i in range(VECTOR_TILES):
                    vector_phi(1, i)
                finish(0, theta_mx, phi_mx, 3)
                quantise_x(2)
                quantise_x2(2)
                scalar_share(2)
                theta_mx = quantise_theta(1)
                phi_mx = quantise_phi(1)
                quantise_x(3)
                quantise_x2(3)
                continue

            ahead = r + QUANTISE_AHEAD
            if ahead < ROUNDS:
                gpsimd_x2(ahead)
            for i in range(VECTOR_TILES):
                vector_phi(r, i)
            for i in range(BATCH_TILES):
                vector_theta(r, i)
            finish(r - 1, theta_mx, phi_mx, ahead)
            if last:
                theta_cols = theta_groups[r][:].rearrange("m c t -> m (c t)")
                half = N * PACK
                phi_mx = quantise_phi(r)
                theta_first = quantise(nc, work, theta_cols[:, :half], N, "theta_first")
            for i in range(BATCH_TILES, TILES - scalar_theta(r)):
                vector_theta(r, i)
            if last:
                theta_second = quantise(nc, work, theta_cols[:, half:], N, "theta_second")
                finish_tiles(0, theta_first, phi_mx)
                finish_tiles(1, theta_second, phi_mx)
                break
            scalar_share(r + 1)
            if scalar_theta(r + 1):
                scalar_tile(theta_w_mx, x_mx[r + 1], theta_bias, theta_groups[r + 1], TILES - 1)
            phi_mx = quantise_phi(r)
            if ahead < ROUNDS:
                quantise_x(ahead)
            theta_mx = quantise_theta(r)
            if ahead < ROUNDS:
                quantise_x2(ahead)
